import numpy as np
import ml_dtypes

BF16 = ml_dtypes.bfloat16


def bf(x):
    return np.asarray(x, np.float32).astype(BF16)


def f32(x):
    return np.asarray(x, np.float32)


def f64(x):
    return np.asarray(x).astype(np.float64)


def striped(idx):
    return np.tile(idx.reshape(-1, 16).T, (8, 1))


C, S, N, HEADS = 512, 4096, 1024, 4
EPS = 1e-5


def norm_all(v):
    return (v - v.mean()) / np.sqrt(v.var() + EPS)


def setup_inputs():
    return {
        "embed": f32(0.8 * np.random.standard_normal((C, S))),
        "pos": f32(0.6 * np.random.standard_normal((C, N))),
        "wp": bf(0.6 * np.random.standard_normal((C, C)) / np.sqrt(C)),
        "bp": f32(0.1 * np.random.standard_normal((C, 1))),
        "wm": bf(1.5 * np.random.standard_normal((HEADS * C, C)) / np.sqrt(HEADS * C)),
        "bm": f32(0.1 + 0.1 * np.random.standard_normal((C, 1))),
        "w1": bf(np.random.standard_normal((C, C)) * np.sqrt(2.0 / C)),
        "b1": f32(0.1 * np.random.standard_normal((C, 1))),
        "w2": bf(np.random.standard_normal((C, C)) / np.sqrt(C)),
        "b2": f32(0.1 + 0.1 * np.random.standard_normal((C, 1))),
        "offs": striped(np.random.permutation(np.tile(np.arange(S), 2))[:N]),
    }


def reference(embed, pos, wp, bp, wm, bm, w1, b1, w2, b2, offs):
    idx = offs[:16].T.reshape(-1)
    h = f64(embed)[:, idx] + f64(pos)
    p = f64(wp).T @ h + f64(bp)
    sc = (p.T @ p) / np.sqrt(C)
    e = np.exp(sc - sc.max(axis=1, keepdims=True))
    a = e / e.sum(axis=1, keepdims=True)
    ctx = p @ a.T
    cat = np.tile(ctx, (HEADS, 1))
    h1 = norm_all(f64(wm).T @ cat + f64(bm) + h)
    f = np.maximum(f64(w1).T @ h1 + f64(b1), 0.0)
    return norm_all(f64(w2).T @ f + f64(b2) + h1)

@@ -1,0 +1,237 @@
+import math
+
+import concourse.mybir as mybir
+from concourse.masks import make_identity
+
+F32 = mybir.dt.float32
+BF16 = mybir.dt.bfloat16
+U16 = mybir.dt.uint16
+ADD = mybir.AluOpType.add
+SUB = mybir.AluOpType.subtract
+MULT = mybir.AluOpType.mult
+MAX = mybir.AluOpType.max
+POW = mybir.AluOpType.pow
+FUNC = mybir.ActivationFunctionType
+X = mybir.AxisListType.X
+
+P = 128
+C = 512
+S = 4096
+N = 1024
+HEADS = 4
+CB = C // P
+NB = N // P
+BANK = 512
+NH = N // BANK
+JB = BANK // P
+EPS = 1e-5
+SCALE = 1.0 / math.sqrt(C)
+
+FLOPS = 2 * (4 * C * C * N + 2 * N * N * C)
+
+
+def tile_trm_b_kernel(tc, embed, pos, wp, bp, wm, bm, w1, b1, w2, b2, offs, out):
+    nc = tc.nc
+
+    def blk(i):
+        return slice(i * P, (i + 1) * P)
+
+    def half(i):
+        return slice(i * BANK, (i + 1) * BANK)
+
+    with (
+        tc.tile_pool(name="held", bufs=1) as held,
+        tc.tile_pool(name="small", bufs=4) as small,
+    ):
+        offsets = held.tile([P, N // 16], U16, name="offsets")
+        nc.sync.dma_start(offsets[:], offs)
+
+        wp_t = held.tile([P, CB, C], BF16, name="wp_t")
+        nc.scalar.dma_start(wp_t[:], wp.rearrange("(a p) d -> p a d", p=P))
+
+        h = [held.tile([P, N], F32, name=f"h{c}") for c in range(CB)]
+        h_bf = [held.tile([P, N], BF16, name=f"h_bf{c}") for c in range(CB)]
+        p_bf = [held.tile([P, N], BF16, name=f"p_bf{d}") for d in range(CB)]
+
+        bias_t = {}
+        wm_t = held.tile([P, HEADS * CB, C], BF16, name="wm_t")
+        w1_t = held.tile([P, CB, C], BF16, name="w1_t")
+        w2_t = held.tile([P, CB, C], BF16, name="w2_t")
+
+        ident = held.tile([P, P], BF16, name="ident")
+        make_identity(nc, ident[:])
+        mean_w = held.tile([P, P], F32, name="mean_w")
+        nc.vector.memset(mean_w[:], 1.0 / (C * N))
+        minus_half = held.tile([P, 1], F32, name="minus_half")
+        nc.vector.memset(minus_half[:], -0.5)
+
+        with (
+            tc.tile_pool(name="table", bufs=1) as table,
+            tc.psum_pool(name="psum_p", bufs=1) as psum_p,
+        ):
+            emb_t = [table.tile([P, S], F32, name=f"emb{c}") for c in range(CB)]
+            pos_t = [table.tile([P, N], F32, name=f"pos{c}") for c in range(CB)]
+            for c in range(CB):
+                nc.sync.dma_start(emb_t[c][:], embed[blk(c), :])
+                nc.scalar.dma_start(pos_t[c][:], pos[blk(c), :])
+            for name, vec in (("bp", bp), ("bm", bm), ("b1", b1), ("b2", b2)):
+                bias_t[name] = held.tile([P, CB], F32, name=name + "_t")
+                nc.scalar.dma_start(bias_t[name][:], vec.rearrange("(a p) o -> p (a o)", p=P))
+            nc.sync.dma_start(wm_t[:], wm.rearrange("(a p) d -> p a d", p=P))
+            nc.sync.dma_start(w1_t[:], w1.rearrange("(a p) d -> p a d", p=P))
+            nc.sync.dma_start(w2_t[:], w2.rearrange("(a p) d -> p a d", p=P))
+
+            p_ps = [[psum_p.tile([P, BANK], F32, name=f"p_ps{d}_{hf}") for hf in range(NH)] for d in range(CB)]
+            for c in range(CB):
+                for hf in range(NH):
+                    picked = emb_t[c][:].indirect(offsets[:, hf * (BANK // 16) : (hf + 1) * (BANK // 16)])
+                    nc.vector.tensor_tensor(h[c][:, half(hf)], picked, pos_t[c][:, half(hf)], ADD)
+                    nc.scalar.copy(h_bf[c][:, half(hf)], h[c][:, half(hf)])
+                    for d in range(CB):
+                        nc.tensor.matmul(
+                            p_ps[d][hf][:], wp_t[:, c, blk(d)], h_bf[c][:, half(hf)],
+                            start=(c == 0), stop=(c == CB - 1),
+                        )
+            for hf in range(NH):
+                for d in range(CB):
+                    if d % 2 == 0:
+                        nc.scalar.activation(
+                            p_bf[d][:, half(hf)], p_ps[d][hf][:], FUNC.Identity, bias=bias_t["bp"][:, d : d + 1]
+                        )
+                    else:
+                        nc.vector.tensor_scalar(
+                            p_bf[d][:, half(hf)], p_ps[d][hf][:], bias_t["bp"][:, d : d + 1], None, op0=ADD
+                        )
+
+        with (
+            tc.tile_pool(name="acts", bufs=1) as acts,
+            tc.tile_pool(name="work", bufs=3) as work,
+            tc.psum_pool(name="psum_mm", bufs=6) as psum_mm,
+            tc.psum_pool(name="psum_tr", bufs=2) as psum_tr,
+        ):
+            pair01 = acts.tile([P, CB, C], F32, name="pair01")
+            pair23 = acts.tile([P, CB, C], F32, name="pair23")
+            wms = acts.tile([P, CB, C], BF16, name="wms")
+            nc.vector.tensor_tensor(pair01[:], wm_t[:, 0:CB, :], wm_t[:, CB : 2 * CB, :], ADD)
+            nc.gpsimd.tensor_tensor(pair23[:], wm_t[:, 2 * CB : 3 * CB, :], wm_t[:, 3 * CB : 4 * CB, :], ADD)
+            nc.vector.tensor_tensor(wms[:], pair01[:], pair23[:], ADD)
+
+            def whole_array_norm(stats, tag):
+                tot = psum_mm.tile([P, BANK], F32, name="tot", tag="mm")
+                k = stats.shape[2]
+                nc.tensor.matmul(tot[:, 0 : 2 * k], mean_w[:], stats[:].rearrange("p s k -> p (s k)"), start=True, stop=True)
+                mom = small.tile([P, 2], F32, name="mom" + tag)
+                nc.vector.tensor_reduce(mom[:], tot[:, 0 : 2 * k].rearrange("p (s k) -> p s k", s=2), axis=X, op=ADD)
+                negvar = small.tile([P, 1], F32, name="negvar" + tag)
+                nc.vector.scalar_tensor_tensor(negvar[:], mom[:, 0:1], mom[:, 0:1], mom[:, 1:2], op0=MULT, op1=SUB)
+                var_eps = small.tile([P, 1], F32, name="var_eps" + tag)
+                nc.vector.tensor_scalar(var_eps[:], negvar[:], -1.0, EPS, op0=MULT, op1=ADD)
+                rstd = small.tile([P, 1], F32, name="rstd" + tag)
+                nc.gpsimd.tensor_tensor(rstd[:], var_eps[:], minus_half[:], POW)
+                shift = small.tile([P, 1], F32, name="shift" + tag)
+                nc.vector.scalar_tensor_tensor(shift[:], mom[:, 0:1], -1.0, rstd[:], op0=MULT, op1=MULT)
+                return rstd, shift
+
+            vT = [acts.tile([P, C], BF16, name=f"vT{t}") for t in range(NB)]
+            aT = [acts.tile([P, NB, BANK], BF16, name=f"aT{hf}") for hf in range(NH)]
+            y = [acts.tile([P, N], F32, name=f"y{c}") for c in range(CB)]
+            y_stats = acts.tile([P, 2, CB * NH], F32, name="y_stats")
+
+            for jb in range(NB):
+                s_ps = [psum_mm.tile([P, BANK], F32, name=f"s_ps{hf}", tag="mm") for hf in range(NH)]
+                for hf in range(NH):
+                    for d in range(CB):
+                        nc.tensor.matmul(
+                            s_ps[hf][:], p_bf[d][:, blk(jb)], p_bf[d][:, half(hf)], start=(d == 0), stop=(d == CB - 1)
+                        )
+                tops = small.tile([P, NH], F32, name="tops")
+                for hf in range(NH):
+                    nc.vector.tensor_reduce(tops[:, hf : hf + 1], s_ps[hf][:], axis=X, op=MAX)
+                neg_top = small.tile([P, 1], F32, name="neg_top")
+                nc.vector.tensor_scalar(neg_top[:], tops[:, 0:1], tops[:, 1:2], -SCALE, op0=MAX, op1=MULT)
+                e = work.tile([P, N], F32, name="e")
+                sums = small.tile([P, NH], F32, name="sums")
+                for hf in range(NH):
+                    nc.scalar.activation(
+                        e[:, half(hf)], s_ps[hf][:], FUNC.Exp, bias=neg_top[:], scale=SCALE,
+                        accum_out=sums[:, hf : hf + 1],
+                    )
+                total = small.tile([P, 1], F32, name="total")
+                nc.vector.tensor_tensor(total[:], sums[:, 0:1], sums[:, 1:2], ADD)
+                inv = small.tile([P, 1], F32, name="inv")
+                nc.vector.reciprocal(inv[:], total[:])
+                a = work.tile([P, N], BF16, name="a")
+                nc.vector.tensor_scalar(a[:], e[:], inv[:], None, op0=MULT)
+
+                v_ps = psum_mm.tile([P, BANK], F32, name="v_ps", tag="mm")
+                for d in range(CB):
+                    nc.tensor.matmul(v_ps[:], p_bf[d][:, blk(jb)], wms[:, d, :], start=(d == 0), stop=(d == CB - 1))
+                nc.scalar.copy(vT[jb][:], v_ps[:])
+
+                a_tr = psum_tr.tile([P, N], BF16, name="a_tr")
+                for tb in range(NB):
+                    nc.tensor.transpose(a_tr[:, blk(tb)], a[:, blk(tb)], ident[:])
+                nc.scalar.copy(aT[jb // JB][:, :, blk(jb % JB)], a_tr[:].rearrange("p (t j) -> p t j", t=NB))
+
+            for hf in range(NH):
+                for c in range(CB):
+                    y_ps = psum_mm.tile([P, BANK], F32, name="y_ps", tag="mm")
+                    for tb in range(NB):
+                        nc.tensor.matmul(y_ps[:], vT[tb][:, blk(c)], aT[hf][:, tb, :], start=(tb == 0), stop=(tb == NB - 1))
+                    k = hf * CB + c
+                    nc.vector.scalar_tensor_tensor(
+                        y[c][:, half(hf)], y_ps[:], bias_t["bm"][:, c : c + 1], h[c][:, half(hf)], op0=ADD, op1=ADD,
+                        accum_out=y_stats[:, 0, k : k + 1],
+                    )
+                    sq = work.tile([P, BANK], BF16, name="sq")
+                    nc.scalar.activation(sq[:], y[c][:, half(hf)], FUNC.Square, accum_out=y_stats[:, 1, k : k + 1])
+
+            rstd1, shift1 = whole_array_norm(y_stats, "1")
+
+            h1_bf = [acts.tile([P, N], BF16, name=f"h1_bf{c}") for c in range(CB)]
+            h1 = [acts.tile([P, N], F32, name=f"h1_{c}") for c in range(CB)]
+            for hf in range(NH):
+                for c in range(CB):
+                    if c % 2 == 0:
+                        nc.vector.tensor_scalar(h1_bf[c][:, half(hf)], y[c][:, half(hf)], rstd1[:], shift1[:], op0=MULT, op1=ADD)
+                    else:
+                        nc.scalar.activation(h1_bf[c][:, half(hf)], y[c][:, half(hf)], FUNC.Identity, bias=shift1[:], scale=rstd1[:])
+            for c in range(CB):
+                nc.gpsimd.tensor_scalar(h1[c][:], y[c][:], rstd1[:], shift1[:], op0=MULT, op1=ADD)
+
+            f_bf = [acts.tile([P, N], BF16, name=f"f_bf{d}") for d in range(CB)]
+            for hf in range(NH):
+                for d in range(CB):
+                    f_ps = psum_mm.tile([P, BANK], F32, name="f_ps", tag="mm")
+                    for c in range(CB):
+                        nc.tensor.matmul(f_ps[:], w1_t[:, c, blk(d)], h1_bf[c][:, half(hf)], start=(c == 0), stop=(c == CB - 1))
+                    if d % 2 == 0:
+                        nc.scalar.activation(f_bf[d][:, half(hf)], f_ps[:], FUNC.Relu, bias=bias_t["b1"][:, d : d + 1])
+                    else:
+                        nc.vector.tensor_scalar(f_bf[d][:, half(hf)], f_ps[:], bias_t["b1"][:, d : d + 1], 0.0, op0=ADD, op1=MAX)
+
+            z = [acts.tile([P, N], F32, name=f"z{c}") for c in range(CB)]
+            z_stats = acts.tile([P, 2, CB * NH], F32, name="z_stats")
+            for hf in range(NH):
+                for c in range(CB):
+                    z_ps = psum_mm.tile([P, BANK], F32, name="z_ps", tag="mm")
+                    for d in range(CB):
+                        nc.tensor.matmul(z_ps[:], w2_t[:, d, blk(c)], f_bf[d][:, half(hf)], start=(d == 0), stop=(d == CB - 1))
+                    k = hf * CB + c
+                    nc.vector.scalar_tensor_tensor(
+                        z[c][:, half(hf)], z_ps[:], bias_t["b2"][:, c : c + 1], h1[c][:, half(hf)], op0=ADD, op1=ADD,
+                        accum_out=z_stats[:, 0, k : k + 1],
+                    )
+                    sq = work.tile([P, BANK], BF16, name="sq")
+                    nc.scalar.activation(sq[:], z[c][:, half(hf)], FUNC.Square, accum_out=z_stats[:, 1, k : k + 1])
+
+            rstd2, shift2 = whole_array_norm(z_stats, "2")
+
+            for c in range(CB):
+                res = acts.tile([P, N], F32, name=f"res{c}")
+                if c % 2 == 0:
+                    nc.vector.tensor_scalar(res[:], z[c][:], rstd2[:], shift2[:], op0=MULT, op1=ADD)
+                    nc.sync.dma_start(out[blk(c), :], res[:])
+                else:
+                    nc.scalar.activation(res[:], z[c][:], FUNC.Identity, bias=shift2[:], scale=rstd2[:])
+                    nc.scalar.dma_start(out[blk(c), :], res[:])

@@ -10,7 +10,6 @@ ADD = mybir.AluOpType.add
 SUB = mybir.AluOpType.subtract
 MULT = mybir.AluOpType.mult
 MAX = mybir.AluOpType.max
-POW = mybir.AluOpType.pow
 FUNC = mybir.ActivationFunctionType
 X = mybir.AxisListType.X
 
@@ -42,12 +41,14 @@ def tile_trm_b_kernel(tc, embed, pos, wp, bp, wm, bm, w1, b1, w2, b2, offs, out)
     with (
         tc.tile_pool(name="held", bufs=1) as held,
         tc.tile_pool(name="small", bufs=4) as small,
+        tc.psum_pool(name="psum_s", bufs=5) as psum_s,
+        tc.psum_pool(name="psum_mm", bufs=2) as psum_mm,
+        tc.psum_pool(name="psum_tr", bufs=1) as psum_tr,
     ):
         offsets = held.tile([P, N // 16], U16, name="offsets")
         nc.sync.dma_start(offsets[:], offs)
 
         wp_t = held.tile([P, CB, C], BF16, name="wp_t")
-        nc.scalar.dma_start(wp_t[:], wp.rearrange("(a p) d -> p a d", p=P))
 
         h = [held.tile([P, N], F32, name=f"h{c}") for c in range(CB)]
         h_bf = [held.tile([P, N], BF16, name=f"h_bf{c}") for c in range(CB)]
@@ -61,19 +62,24 @@ def tile_trm_b_kernel(tc, embed, pos, wp, bp, wm, bm, w1, b1, w2, b2, offs, out)
         ident = held.tile([P, P], BF16, name="ident")
         make_identity(nc, ident[:])
         mean_w = held.tile([P, P], F32, name="mean_w")
-        nc.vector.memset(mean_w[:], 1.0 / (C * N))
-        minus_half = held.tile([P, 1], F32, name="minus_half")
-        nc.vector.memset(minus_half[:], -0.5)
+        nc.vector.memset(mean_w[:], -1.0 / (C * N))
+        half_mean_w = held.tile([P, P], F32, name="half_mean_w")
+        nc.vector.memset(half_mean_w[:], -1.0 / (C * BANK))
+        ones_bf = held.tile([P, 1], BF16, name="ones_bf")
+        nc.vector.memset(ones_bf[:], 1.0)
+        eps_t = held.tile([P, 1], F32, name="eps_t")
+        nc.vector.memset(eps_t[:], EPS)
+        warm = held.tile([P, 1], F32, name="warm")
+        nc.scalar.activation(warm[:], eps_t[:], FUNC.Exp)
 
-        with (
-            tc.tile_pool(name="table", bufs=1) as table,
-            tc.psum_pool(name="psum_p", bufs=1) as psum_p,
-        ):
+        with tc.tile_pool(name="table", bufs=1) as table:
             emb_t = [table.tile([P, S], F32, name=f"emb{c}") for c in range(CB)]
             pos_t = [table.tile([P, N], F32, name=f"pos{c}") for c in range(CB)]
             for c in range(CB):
+                if c == CB - 1:
+                    nc.sync.dma_start(wp_t[:], wp.rearrange("(a p) d -> p a d", p=P))
                 nc.sync.dma_start(emb_t[c][:], embed[blk(c), :])
-                nc.scalar.dma_start(pos_t[c][:], pos[blk(c), :])
+                nc.sync.dma_start(pos_t[c][:], pos[blk(c), :])
             for name, vec in (("bp", bp), ("bm", bm), ("b1", b1), ("b2", b2)):
                 bias_t[name] = held.tile([P, CB], F32, name=name + "_t")
                 nc.scalar.dma_start(bias_t[name][:], vec.rearrange("(a p) o -> p (a o)", p=P))
@@ -81,7 +87,11 @@ def tile_trm_b_kernel(tc, embed, pos, wp, bp, wm, bm, w1, b1, w2, b2, offs, out)
             nc.sync.dma_start(w1_t[:], w1.rearrange("(a p) d -> p a d", p=P))
             nc.sync.dma_start(w2_t[:], w2.rearrange("(a p) d -> p a d", p=P))
 
-            p_ps = [[psum_p.tile([P, BANK], F32, name=f"p_ps{d}_{hf}") for hf in range(NH)] for d in range(CB)]
+            lenders = [(psum_s, "s")] * 5 + [(psum_mm, "mm")] * 2 + [(psum_tr, "tr")]
+            p_ps = [
+                [lenders[hf * CB + d][0].tile([P, BANK], F32, name=f"p_ps{d}_{hf}", tag=lenders[hf * CB + d][1]) for hf in range(NH)]
+                for d in range(CB)
+            ]
             for c in range(CB):
                 for hf in range(NH):
                     picked = emb_t[c][:].indirect(offsets[:, hf * (BANK // 16) : (hf + 1) * (BANK // 16)])
@@ -106,39 +116,39 @@ def tile_trm_b_kernel(tc, embed, pos, wp, bp, wm, bm, w1, b1, w2, b2, offs, out)
         with (
             tc.tile_pool(name="acts", bufs=1) as acts,
             tc.tile_pool(name="work", bufs=3) as work,
-            tc.psum_pool(name="psum_mm", bufs=6) as psum_mm,
-            tc.psum_pool(name="psum_tr", bufs=2) as psum_tr,
         ):
             pair01 = acts.tile([P, CB, C], F32, name="pair01")
             pair23 = acts.tile([P, CB, C], F32, name="pair23")
             wms = acts.tile([P, CB, C], BF16, name="wms")
-            nc.vector.tensor_tensor(pair01[:], wm_t[:, 0:CB, :], wm_t[:, CB : 2 * CB, :], ADD)
+            nc.gpsimd.tensor_tensor(pair01[:], wm_t[:, 0:CB, :], wm_t[:, CB : 2 * CB, :], ADD)
             nc.gpsimd.tensor_tensor(pair23[:], wm_t[:, 2 * CB : 3 * CB, :], wm_t[:, 3 * CB : 4 * CB, :], ADD)
-            nc.vector.tensor_tensor(wms[:], pair01[:], pair23[:], ADD)
+            nc.gpsimd.tensor_tensor(wms[:], pair01[:], pair23[:], ADD)
 
             def whole_array_norm(stats, tag):
-                tot = psum_mm.tile([P, BANK], F32, name="tot", tag="mm")
+                tot = psum_tr.tile([P, BANK], F32, name="tot", tag="tr")
                 k = stats.shape[2]
                 nc.tensor.matmul(tot[:, 0 : 2 * k], mean_w[:], stats[:].rearrange("p s k -> p (s k)"), start=True, stop=True)
                 mom = small.tile([P, 2], F32, name="mom" + tag)
                 nc.vector.tensor_reduce(mom[:], tot[:, 0 : 2 * k].rearrange("p (s k) -> p s k", s=2), axis=X, op=ADD)
                 negvar = small.tile([P, 1], F32, name="negvar" + tag)
-                nc.vector.scalar_tensor_tensor(negvar[:], mom[:, 0:1], mom[:, 0:1], mom[:, 1:2], op0=MULT, op1=SUB)
-                var_eps = small.tile([P, 1], F32, name="var_eps" + tag)
-                nc.vector.tensor_scalar(var_eps[:], negvar[:], -1.0, EPS, op0=MULT, op1=ADD)
+                nc.vector.scalar_tensor_tensor(negvar[:], mom[:, 0:1], mom[:, 0:1], mom[:, 1:2], op0=MULT, op1=ADD)
+                sigma = small.tile([P, 1], F32, name="sigma" + tag)
+                nc.scalar.activation(sigma[:], negvar[:], FUNC.Sqrt, bias=eps_t[:], scale=-1.0)
                 rstd = small.tile([P, 1], F32, name="rstd" + tag)
-                nc.gpsimd.tensor_tensor(rstd[:], var_eps[:], minus_half[:], POW)
+                nc.vector.reciprocal(rstd[:], sigma[:])
                 shift = small.tile([P, 1], F32, name="shift" + tag)
-                nc.vector.scalar_tensor_tensor(shift[:], mom[:, 0:1], -1.0, rstd[:], op0=MULT, op1=MULT)
-                return rstd, shift
+                nc.vector.tensor_tensor(shift[:], mom[:, 0:1], rstd[:], MULT)
+                return mom[:, 0:1], sigma, rstd, shift
 
             vT = [acts.tile([P, C], BF16, name=f"vT{t}") for t in range(NB)]
             aT = [acts.tile([P, NB, BANK], BF16, name=f"aT{hf}") for hf in range(NH)]
             y = [acts.tile([P, N], F32, name=f"y{c}") for c in range(CB)]
             y_stats = acts.tile([P, 2, CB * NH], F32, name="y_stats")
 
-            for jb in range(NB):
-                s_ps = [psum_mm.tile([P, BANK], F32, name=f"s_ps{hf}", tag="mm") for hf in range(NH)]
+            e_of, sums_of, a_of = {}, {}, {}
+
+            def scores_and_exp(jb):
+                s_ps = [psum_s.tile([P, BANK], F32, name=f"s_ps{hf}", tag="s") for hf in range(NH)]
                 for hf in range(NH):
                     for d in range(CB):
                         nc.tensor.matmul(
@@ -149,89 +159,139 @@ def tile_trm_b_kernel(tc, embed, pos, wp, bp, wm, bm, w1, b1, w2, b2, offs, out)
                     nc.vector.tensor_reduce(tops[:, hf : hf + 1], s_ps[hf][:], axis=X, op=MAX)
                 neg_top = small.tile([P, 1], F32, name="neg_top")
                 nc.vector.tensor_scalar(neg_top[:], tops[:, 0:1], tops[:, 1:2], -SCALE, op0=MAX, op1=MULT)
-                e = work.tile([P, N], F32, name="e")
-                sums = small.tile([P, NH], F32, name="sums")
+                e_of[jb] = work.tile([P, N], F32, name="e")
+                sums_of[jb] = small.tile([P, NH], F32, name="sums")
                 for hf in range(NH):
                     nc.scalar.activation(
-                        e[:, half(hf)], s_ps[hf][:], FUNC.Exp, bias=neg_top[:], scale=SCALE,
-                        accum_out=sums[:, hf : hf + 1],
+                        e_of[jb][:, half(hf)], s_ps[hf][:], FUNC.Exp, bias=neg_top[:], scale=SCALE,
+                        accum_out=sums_of[jb][:, hf : hf + 1],
                     )
+
+            def normalise(jb):
                 total = small.tile([P, 1], F32, name="total")
-                nc.vector.tensor_tensor(total[:], sums[:, 0:1], sums[:, 1:2], ADD)
+                nc.vector.tensor_tensor(total[:], sums_of[jb][:, 0:1], sums_of[jb][:, 1:2], ADD)
                 inv = small.tile([P, 1], F32, name="inv")
                 nc.vector.reciprocal(inv[:], total[:])
-                a = work.tile([P, N], BF16, name="a")
-                nc.vector.tensor_scalar(a[:], e[:], inv[:], None, op0=MULT)
+                a_of[jb] = work.tile([P, N], BF16, name="a")
+                nc.scalar.activation(a_of[jb][:], e_of[jb][:], FUNC.Identity, scale=inv[:])
 
+            def transpose_weights(jb):
+                a_tr = psum_tr.tile([P, N], BF16, name="a_tr", tag="tr")
+                for tb in range(NB):
+                    nc.tensor.transpose(a_tr[:, blk(tb)], a_of[jb][:, blk(tb)], ident[:])
+                nc.vector.tensor_copy(aT[jb // JB][:, :, blk(jb % JB)], a_tr[:].rearrange("p (t j) -> p t j", t=NB))
+
+            def v_block(tb):
                 v_ps = psum_mm.tile([P, BANK], F32, name="v_ps", tag="mm")
                 for d in range(CB):
-                    nc.tensor.matmul(v_ps[:], p_bf[d][:, blk(jb)], wms[:, d, :], start=(d == 0), stop=(d == CB - 1))
-                nc.scalar.copy(vT[jb][:], v_ps[:])
+                    nc.tensor.matmul(v_ps[:], p_bf[d][:, blk(tb)], wms[:, d, :], start=(d == 0), stop=(d == CB - 1))
+                if tb % 2 == 0:
+                    nc.scalar.copy(vT[tb][:], v_ps[:])
+                else:
+                    nc.vector.tensor_copy(vT[tb][:], v_ps[:])
 
-                a_tr = psum_tr.tile([P, N], BF16, name="a_tr")
+            for step in range(NB + 2):
+                if step < NB:
+                    scores_and_exp(step)
+                else:
+                    v_block(2 * (step - NB))
+                    v_block(2 * (step - NB) + 1)
+                if 1 <= step <= NB:
+                    normalise(step - 1)
+                if step >= 2:
+                    transpose_weights(step - 2)
+            for tb in range(4, NB):
+                v_block(tb)
+
+            cs_ps = psum_tr.tile([P, BANK], F32, name="cs_ps", tag="tr")
+            for d in range(CB):
+                for c in range(CB):
+                    nc.tensor.matmul(cs_ps[:, d : d + 1], w1_t[:, c, blk(d)], ones_bf[:], start=(c == 0), stop=(c == CB - 1))
+            w1_colsum = acts.tile([P, CB], F32, name="w1_colsum")
+            nc.vector.tensor_copy(w1_colsum[:], cs_ps[:, 0:CB])
+
+            yc_bf = [acts.tile([P, N], BF16, name=f"yc_bf{c}") for c in range(CB)]
+            neg_m0 = acts.tile([P, 1], F32, name="neg_m0")
+
+            def centre(hf, c):
+                nc.gpsimd.tensor_scalar(yc_bf[c][:, half(hf)], y[c][:, half(hf)], 1.0, neg_m0[:], op0=MULT, op1=ADD)
+
+            for k in range(NH * CB):
+                hf, c = divmod(k, CB)
+                y_ps = psum_mm.tile([P, BANK], F32, name="y_ps", tag="mm")
                 for tb in range(NB):
-                    nc.tensor.transpose(a_tr[:, blk(tb)], a[:, blk(tb)], ident[:])
-                nc.scalar.copy(aT[jb // JB][:, :, blk(jb % JB)], a_tr[:].rearrange("p (t j) -> p t j", t=NB))
-
-            for hf in range(NH):
-                for c in range(CB):
-                    y_ps = psum_mm.tile([P, BANK], F32, name="y_ps", tag="mm")
-                    for tb in range(NB):
-                        nc.tensor.matmul(y_ps[:], vT[tb][:, blk(c)], aT[hf][:, tb, :], start=(tb == 0), stop=(tb == NB - 1))
-                    k = hf * CB + c
-                    nc.vector.scalar_tensor_tensor(
-                        y[c][:, half(hf)], y_ps[:], bias_t["bm"][:, c : c + 1], h[c][:, half(hf)], op0=ADD, op1=ADD,
-                        accum_out=y_stats[:, 0, k : k + 1],
-                    )
-                    sq = work.tile([P, BANK], BF16, name="sq")
-                    nc.scalar.activation(sq[:], y[c][:, half(hf)], FUNC.Square, accum_out=y_stats[:, 1, k : k + 1])
-
-            rstd1, shift1 = whole_array_norm(y_stats, "1")
-
-            h1_bf = [acts.tile([P, N], BF16, name=f"h1_bf{c}") for c in range(CB)]
-            h1 = [acts.tile([P, N], F32, name=f"h1_{c}") for c in range(CB)]
-            for hf in range(NH):
-                for c in range(CB):
-                    if c % 2 == 0:
-                        nc.vector.tensor_scalar(h1_bf[c][:, half(hf)], y[c][:, half(hf)], rstd1[:], shift1[:], op0=MULT, op1=ADD)
-                    else:
-                        nc.scalar.activation(h1_bf[c][:, half(hf)], y[c][:, half(hf)], FUNC.Identity, bias=shift1[:], scale=rstd1[:])
-            for c in range(CB):
-                nc.gpsimd.tensor_scalar(h1[c][:], y[c][:], rstd1[:], shift1[:], op0=MULT, op1=ADD)
+                    nc.tensor.matmul(y_ps[:], vT[tb][:, blk(c)], aT[hf][:, tb, :], start=(tb == 0), stop=(tb == NB - 1))
+                if k == CB:
+                    m0_ps = psum_tr.tile([P, BANK], F32, name="m0_ps", tag="tr")
+                    nc.tensor.matmul(m0_ps[:, 0:CB], half_mean_w[:], y_stats[:, 0, 0:CB], start=True, stop=True)
+                    nc.vector.tensor_reduce(neg_m0[:], m0_ps[:, 0:CB], axis=X, op=ADD)
+                    for c0 in range(CB):
+                        centre(0, c0)
+                nc.vector.scalar_tensor_tensor(
+                    y[c][:, half(hf)], y_ps[:], bias_t["bm"][:, c : c + 1], h[c][:, half(hf)], op0=ADD, op1=ADD,
+                    accum_out=y_stats[:, 0, k : k + 1],
+                )
+                sq = work.tile([P, BANK], BF16, name="sq")
+                nc.scalar.activation(sq[:], y[c][:, half(hf)], FUNC.Square, accum_out=y_stats[:, 1, k : k + 1])
+                if hf == 1:
+                    centre(1, c)
 
             f_bf = [acts.tile([P, N], BF16, name=f"f_bf{d}") for d in range(CB)]
-            for hf in range(NH):
-                for d in range(CB):
-                    f_ps = psum_mm.tile([P, BANK], F32, name="f_ps", tag="mm")
-                    for c in range(CB):
-                        nc.tensor.matmul(f_ps[:], w1_t[:, c, blk(d)], h1_bf[c][:, half(hf)], start=(c == 0), stop=(c == CB - 1))
-                    if d % 2 == 0:
-                        nc.scalar.activation(f_bf[d][:, half(hf)], f_ps[:], FUNC.Relu, bias=bias_t["b1"][:, d : d + 1])
-                    else:
-                        nc.vector.tensor_scalar(f_bf[d][:, half(hf)], f_ps[:], bias_t["b1"][:, d : d + 1], 0.0, op0=ADD, op1=MAX)
+
+            def f_products(k):
+                hf, d = divmod(k, CB)
+                f_ps = psum_s.tile([P, BANK], F32, name="f_ps", tag="s")
+                for c in range(CB):
+                    nc.tensor.matmul(f_ps[:], w1_t[:, c, blk(d)], yc_bf[c][:, half(hf)], start=(c == 0), stop=(c == CB - 1))
+                return f_ps
+
+            AHEAD = 2
+            f_early = [f_products(k) for k in range(AHEAD)]
+
+            neg_mean1, sigma1, rstd1, shift1 = whole_array_norm(y_stats, "1")
+            drift = small.tile([P, 1], F32, name="drift")
+            nc.vector.tensor_tensor(drift[:], neg_mean1, neg_m0[:], SUB)
+            drift_cs = small.tile([P, CB], F32, name="drift_cs")
+            nc.vector.tensor_scalar(drift_cs[:], w1_colsum[:], drift[:], None, op0=MULT)
+            f_bias = small.tile([P, CB], F32, name="f_bias")
+            nc.vector.scalar_tensor_tensor(f_bias[:], bias_t["b1"][:], sigma1[:], drift_cs[:], op0=MULT, op1=ADD)
+            shift_b2 = small.tile([P, CB], F32, name="shift_b2")
+            nc.vector.tensor_scalar(shift_b2[:], bias_t["b2"][:], shift1[:], None, op0=ADD)
+
+            for k in range(NH * CB):
+                hf, d = divmod(k, CB)
+                f_ps = f_early[k] if k < AHEAD else f_products(k)
+                if d % 2 == 0:
+                    nc.scalar.activation(f_bf[d][:, half(hf)], f_ps[:], FUNC.Relu, bias=f_bias[:, d : d + 1])
+                else:
+                    nc.vector.tensor_scalar(f_bf[d][:, half(hf)], f_ps[:], f_bias[:, d : d + 1], 0.0, op0=ADD, op1=MAX)
+
+            h1_b2 = [acts.tile([P, N], F32, name=f"h1_b2_{c}") for c in range(CB)]
+            for c in range(CB):
+                nc.gpsimd.tensor_scalar(h1_b2[c][:], y[c][:], rstd1[:], shift_b2[:, c : c + 1], op0=MULT, op1=ADD)
 
             z = [acts.tile([P, N], F32, name=f"z{c}") for c in range(CB)]
             z_stats = acts.tile([P, 2, CB * NH], F32, name="z_stats")
-            for hf in range(NH):
-                for c in range(CB):
-                    z_ps = psum_mm.tile([P, BANK], F32, name="z_ps", tag="mm")
-                    for d in range(CB):
-                        nc.tensor.matmul(z_ps[:], w2_t[:, d, blk(c)], f_bf[d][:, half(hf)], start=(d == 0), stop=(d == CB - 1))
-                    k = hf * CB + c
-                    nc.vector.scalar_tensor_tensor(
-                        z[c][:, half(hf)], z_ps[:], bias_t["b2"][:, c : c + 1], h1[c][:, half(hf)], op0=ADD, op1=ADD,
-                        accum_out=z_stats[:, 0, k : k + 1],
-                    )
-                    sq = work.tile([P, BANK], BF16, name="sq")
-                    nc.scalar.activation(sq[:], z[c][:, half(hf)], FUNC.Square, accum_out=z_stats[:, 1, k : k + 1])
+            for k in range(NH * CB):
+                hf, c = divmod(k, CB)
+                z_ps = psum_mm.tile([P, BANK], F32, name="z_ps", tag="mm")
+                for d in range(CB):
+                    nc.tensor.matmul(z_ps[:], w2_t[:, d, blk(c)], f_bf[d][:, half(hf)], start=(d == 0), stop=(d == CB - 1))
+                nc.vector.scalar_tensor_tensor(
+                    z[c][:, half(hf)], z_ps[:], rstd1[:], h1_b2[c][:, half(hf)], op0=MULT, op1=ADD,
+                    accum_out=z_stats[:, 0, k : k + 1],
+                )
+                sq = work.tile([P, BANK], BF16, name="sq")
+                nc.scalar.activation(sq[:], z[c][:, half(hf)], FUNC.Square, accum_out=z_stats[:, 1, k : k + 1])
 
-            rstd2, shift2 = whole_array_norm(z_stats, "2")
+            neg_mean2, sigma2, rstd2, shift2 = whole_array_norm(z_stats, "2")
 
+            res = [acts.tile([P, N], F32, name=f"res{c}") for c in range(CB)]
             for c in range(CB):
-                res = acts.tile([P, N], F32, name=f"res{c}")
-                if c % 2 == 0:
-                    nc.vector.tensor_scalar(res[:], z[c][:], rstd2[:], shift2[:], op0=MULT, op1=ADD)
-                    nc.sync.dma_start(out[blk(c), :], res[:])
-                else:
-                    nc.scalar.activation(res[:], z[c][:], FUNC.Identity, bias=shift2[:], scale=rstd2[:])
-                    nc.scalar.dma_start(out[blk(c), :], res[:])
+                for hf in range(NH):
+                    if (c * NH + hf) % 3 < 2:
+                        nc.vector.tensor_scalar(res[c][:, half(hf)], z[c][:, half(hf)], neg_mean2, rstd2[:], op0=ADD, op1=MULT)
+                        nc.sync.dma_start(out[blk(c), half(hf)], res[c][:, half(hf)])
+                    else:
+                        nc.scalar.activation(res[c][:, half(hf)], z[c][:, half(hf)], FUNC.Identity, bias=shift2[:], scale=rstd2[:])
+                        nc.scalar.dma_start(out[blk(c), half(hf)], res[c][:, half(hf)])

@@ -54,7 +54,8 @@ def tile_trm_b_kernel(tc, embed, pos, wp, bp, wm, bm, w1, b1, w2, b2, offs, out)
         h_bf = [held.tile([P, N], BF16, name=f"h_bf{c}") for c in range(CB)]
         p_bf = [held.tile([P, N], BF16, name=f"p_bf{d}") for d in range(CB)]
 
-        bias_t = {}
+        bias_t = {"bp": held.tile([P, CB], F32, name="bp_t")}
+        nc.scalar.dma_start(bias_t["bp"][:], bp.rearrange("(a p) o -> p (a o)", p=P))
         wm_t = held.tile([P, HEADS * CB, C], BF16, name="wm_t")
         w1_t = held.tile([P, CB, C], BF16, name="w1_t")
         w2_t = held.tile([P, CB, C], BF16, name="w2_t")
@@ -80,12 +81,12 @@ def tile_trm_b_kernel(tc, embed, pos, wp, bp, wm, bm, w1, b1, w2, b2, offs, out)
                     nc.sync.dma_start(wp_t[:], wp.rearrange("(a p) d -> p a d", p=P))
                 nc.sync.dma_start(emb_t[c][:], embed[blk(c), :])
                 nc.sync.dma_start(pos_t[c][:], pos[blk(c), :])
-            for name, vec in (("bp", bp), ("bm", bm), ("b1", b1), ("b2", b2)):
-                bias_t[name] = held.tile([P, CB], F32, name=name + "_t")
-                nc.scalar.dma_start(bias_t[name][:], vec.rearrange("(a p) o -> p (a o)", p=P))
             nc.sync.dma_start(wm_t[:], wm.rearrange("(a p) d -> p a d", p=P))
             nc.sync.dma_start(w1_t[:], w1.rearrange("(a p) d -> p a d", p=P))
             nc.sync.dma_start(w2_t[:], w2.rearrange("(a p) d -> p a d", p=P))
+            for name, vec in (("bm", bm), ("b1", b1), ("b2", b2)):
+                bias_t[name] = held.tile([P, CB], F32, name=name + "_t")
+                nc.sync.dma_start(bias_t[name][:], vec.rearrange("(a p) o -> p (a o)", p=P))
 
             lenders = [(psum_s, "s")] * 5 + [(psum_mm, "mm")] * 2 + [(psum_tr, "tr")]
             p_ps = [
@@ -120,9 +121,10 @@ def tile_trm_b_kernel(tc, embed, pos, wp, bp, wm, bm, w1, b1, w2, b2, offs, out)
             pair01 = acts.tile([P, CB, C], F32, name="pair01")
             pair23 = acts.tile([P, CB, C], F32, name="pair23")
             wms = acts.tile([P, CB, C], BF16, name="wms")
-            nc.gpsimd.tensor_tensor(pair01[:], wm_t[:, 0:CB, :], wm_t[:, CB : 2 * CB, :], ADD)
-            nc.gpsimd.tensor_tensor(pair23[:], wm_t[:, 2 * CB : 3 * CB, :], wm_t[:, 3 * CB : 4 * CB, :], ADD)
-            nc.gpsimd.tensor_tensor(wms[:], pair01[:], pair23[:], ADD)
+            for d in range(CB):
+                nc.gpsimd.tensor_tensor(pair01[:, d, :], wm_t[:, d, :], wm_t[:, CB + d, :], ADD)
+                nc.gpsimd.tensor_tensor(pair23[:, d, :], wm_t[:, 2 * CB + d, :], wm_t[:, 3 * CB + d, :], ADD)
+                nc.gpsimd.tensor_tensor(wms[:, d, :], pair01[:, d, :], pair23[:, d, :], ADD)
 
             def whole_array_norm(stats, tag):
                 tot = psum_tr.tile([P, BANK], F32, name="tot", tag="tr")
@@ -131,13 +133,13 @@ def tile_trm_b_kernel(tc, embed, pos, wp, bp, wm, bm, w1, b1, w2, b2, offs, out)
                 mom = small.tile([P, 2], F32, name="mom" + tag)
                 nc.vector.tensor_reduce(mom[:], tot[:, 0 : 2 * k].rearrange("p (s k) -> p s k", s=2), axis=X, op=ADD)
                 negvar = small.tile([P, 1], F32, name="negvar" + tag)
-                nc.vector.scalar_tensor_tensor(negvar[:], mom[:, 0:1], mom[:, 0:1], mom[:, 1:2], op0=MULT, op1=ADD)
+                nc.vector.tensor_scalar(negvar[:], mom[:, 0:1], mom[:, 0:1], mom[:, 1:2], op0=MULT, op1=ADD)
                 sigma = small.tile([P, 1], F32, name="sigma" + tag)
                 nc.scalar.activation(sigma[:], negvar[:], FUNC.Sqrt, bias=eps_t[:], scale=-1.0)
                 rstd = small.tile([P, 1], F32, name="rstd" + tag)
                 nc.vector.reciprocal(rstd[:], sigma[:])
                 shift = small.tile([P, 1], F32, name="shift" + tag)
-                nc.vector.tensor_tensor(shift[:], mom[:, 0:1], rstd[:], MULT)
+                nc.vector.tensor_scalar(shift[:], mom[:, 0:1], rstd[:], None, op0=MULT)
                 return mom[:, 0:1], sigma, rstd, shift
 
             vT = [acts.tile([P, C], BF16, name=f"vT{t}") for t in range(NB)]
@@ -169,7 +171,7 @@ def tile_trm_b_kernel(tc, embed, pos, wp, bp, wm, bm, w1, b1, w2, b2, offs, out)
 
             def normalise(jb):
                 total = small.tile([P, 1], F32, name="total")
-                nc.vector.tensor_tensor(total[:], sums_of[jb][:, 0:1], sums_of[jb][:, 1:2], ADD)
+                nc.vector.tensor_reduce(total[:], sums_of[jb][:], axis=X, op=ADD)
                 inv = small.tile([P, 1], F32, name="inv")
                 nc.vector.reciprocal(inv[:], total[:])
                 a_of[jb] = work.tile([P, N], BF16, name="a")
@@ -250,7 +252,7 @@ def tile_trm_b_kernel(tc, embed, pos, wp, bp, wm, bm, w1, b1, w2, b2, offs, out)
 
             neg_mean1, sigma1, rstd1, shift1 = whole_array_norm(y_stats, "1")
             drift = small.tile([P, 1], F32, name="drift")
-            nc.vector.tensor_tensor(drift[:], neg_mean1, neg_m0[:], SUB)
+            nc.vector.tensor_scalar(drift[:], neg_mean1, neg_m0[:], None, op0=SUB)
             drift_cs = small.tile([P, CB], F32, name="drift_cs")
             nc.vector.tensor_scalar(drift_cs[:], w1_colsum[:], drift[:], None, op0=MULT)
             f_bias = small.tile([P, CB], F32, name="f_bias")

@@ -23,6 +23,7 @@ NB = N // P
 BANK = 512
 NH = N // BANK
 JB = BANK // P
+BIAS_ROWS = 64
 EPS = 1e-5
 SCALE = 1.0 / math.sqrt(C)
 
@@ -54,8 +55,6 @@ def tile_trm_b_kernel(tc, embed, pos, wp, bp, wm, bm, w1, b1, w2, b2, offs, out)
         h_bf = [held.tile([P, N], BF16, name=f"h_bf{c}") for c in range(CB)]
         p_bf = [held.tile([P, N], BF16, name=f"p_bf{d}") for d in range(CB)]
 
-        bias_t = {"bp": held.tile([P, CB], F32, name="bp_t")}
-        nc.scalar.dma_start(bias_t["bp"][:], bp.rearrange("(a p) o -> p (a o)", p=P))
         wm_t = held.tile([P, HEADS * CB, C], BF16, name="wm_t")
         w1_t = held.tile([P, CB, C], BF16, name="w1_t")
         w2_t = held.tile([P, CB, C], BF16, name="w2_t")
@@ -73,6 +72,18 @@ def tile_trm_b_kernel(tc, embed, pos, wp, bp, wm, bm, w1, b1, w2, b2, offs, out)
         warm = held.tile([P, 1], F32, name="warm")
         nc.scalar.activation(warm[:], eps_t[:], FUNC.Exp)
 
+        bias_rows = held.tile([BIAS_ROWS, P], F32, name="bias_rows")
+        nc.vector.memset(bias_rows[:], 0.0)
+        for i, vec in enumerate((bp, bm, b1, b2)):
+            nc.scalar.dma_start(bias_rows[i * CB : (i + 1) * CB, :], vec.rearrange("(a p) o -> a (p o)", p=P))
+        ident_f = held.tile([BIAS_ROWS, BIAS_ROWS], F32, name="ident_f")
+        make_identity(nc, ident_f[:])
+        bias_ps = psum_tr.tile([P, BANK], F32, name="bias_ps", tag="tr")
+        nc.tensor.transpose(bias_ps[:, 0:BIAS_ROWS], bias_rows[:], ident_f[:])
+        bias_cols = held.tile([P, 4 * CB], F32, name="bias_cols")
+        nc.vector.tensor_copy(bias_cols[:], bias_ps[:, 0 : 4 * CB])
+        bias_t = {name: bias_cols[:, i * CB : (i + 1) * CB] for i, name in enumerate(("bp", "bm", "b1", "b2"))}
+
         with tc.tile_pool(name="table", bufs=1) as table:
             emb_t = [table.tile([P, S], F32, name=f"emb{c}") for c in range(CB)]
             pos_t = [table.tile([P, N], F32, name=f"pos{c}") for c in range(CB)]
@@ -84,9 +95,6 @@ def tile_trm_b_kernel(tc, embed, pos, wp, bp, wm, bm, w1, b1, w2, b2, offs, out)
             nc.sync.dma_start(wm_t[:], wm.rearrange("(a p) d -> p a d", p=P))
             nc.sync.dma_start(w1_t[:], w1.rearrange("(a p) d -> p a d", p=P))
             nc.sync.dma_start(w2_t[:], w2.rearrange("(a p) d -> p a d", p=P))
-            for name, vec in (("bm", bm), ("b1", b1), ("b2", b2)):
-                bias_t[name] = held.tile([P, CB], F32, name=name + "_t")
-                nc.sync.dma_start(bias_t[name][:], vec.rearrange("(a p) o -> p (a o)", p=P))
 
             lenders = [(psum_s, "s")] * 5 + [(psum_mm, "mm")] * 2 + [(psum_tr, "tr")]
             p_ps = [
@@ -256,9 +264,9 @@ def tile_trm_b_kernel(tc, embed, pos, wp, bp, wm, bm, w1, b1, w2, b2, offs, out)
             drift_cs = small.tile([P, CB], F32, name="drift_cs")
             nc.vector.tensor_scalar(drift_cs[:], w1_colsum[:], drift[:], None, op0=MULT)
             f_bias = small.tile([P, CB], F32, name="f_bias")
-            nc.vector.scalar_tensor_tensor(f_bias[:], bias_t["b1"][:], sigma1[:], drift_cs[:], op0=MULT, op1=ADD)
+            nc.vector.scalar_tensor_tensor(f_bias[:], bias_t["b1"], sigma1[:], drift_cs[:], op0=MULT, op1=ADD)
             shift_b2 = small.tile([P, CB], F32, name="shift_b2")
-            nc.vector.tensor_scalar(shift_b2[:], bias_t["b2"][:], shift1[:], None, op0=ADD)
+            nc.vector.tensor_scalar(shift_b2[:], bias_t["b2"], shift1[:], None, op0=ADD)
 
             for k in range(NH * CB):
                 hf, d = divmod(k, CB)

@@ -23,9 +23,19 @@ NB = N // P
 BANK = 512
 NH = N // BANK
 JB = BANK // P
-BIAS_ROWS = 64
+GROUPS = NH * CB
 EPS = 1e-5
 SCALE = 1.0 / math.sqrt(C)
+
+S_BANKS = 5
+Y_BANKS = 2
+T_BANKS = 1
+
+BIAS_ROWS = 64
+LAG_B = 1
+LAG_C = 2
+V_IN_DRAIN = 2
+AHEAD = 2
 
 FLOPS = 2 * (4 * C * C * N + 2 * N * N * C)
 
@@ -42,22 +52,20 @@ def tile_trm_b_kernel(tc, embed, pos, wp, bp, wm, bm, w1, b1, w2, b2, offs, out)
     with (
         tc.tile_pool(name="held", bufs=1) as held,
         tc.tile_pool(name="small", bufs=4) as small,
-        tc.psum_pool(name="psum_s", bufs=5) as psum_s,
-        tc.psum_pool(name="psum_mm", bufs=2) as psum_mm,
-        tc.psum_pool(name="psum_tr", bufs=1) as psum_tr,
+        tc.psum_pool(name="psum_s", bufs=S_BANKS) as psum_s,
+        tc.psum_pool(name="psum_y", bufs=Y_BANKS) as psum_y,
+        tc.psum_pool(name="psum_t", bufs=T_BANKS) as psum_t,
     ):
         offsets = held.tile([P, N // 16], U16, name="offsets")
         nc.sync.dma_start(offsets[:], offs)
 
         wp_t = held.tile([P, CB, C], BF16, name="wp_t")
-
-        h = [held.tile([P, N], F32, name=f"h{c}") for c in range(CB)]
-        h_bf = [held.tile([P, N], BF16, name=f"h_bf{c}") for c in range(CB)]
-        p_bf = [held.tile([P, N], BF16, name=f"p_bf{d}") for d in range(CB)]
-
         wm_t = held.tile([P, HEADS * CB, C], BF16, name="wm_t")
         w1_t = held.tile([P, CB, C], BF16, name="w1_t")
         w2_t = held.tile([P, CB, C], BF16, name="w2_t")
+        h = [held.tile([P, N], F32, name=f"h{c}") for c in range(CB)]
+        h_bf = [held.tile([P, N], BF16, name=f"h_bf{c}") for c in range(CB)]
+        p_bf = [held.tile([P, N], BF16, name=f"p_bf{d}") for d in range(CB)]
 
         ident = held.tile([P, P], BF16, name="ident")
         make_identity(nc, ident[:])
@@ -75,32 +83,35 @@ def tile_trm_b_kernel(tc, embed, pos, wp, bp, wm, bm, w1, b1, w2, b2, offs, out)
         bias_rows = held.tile([BIAS_ROWS, P], F32, name="bias_rows")
         nc.vector.memset(bias_rows[:], 0.0)
         for i, vec in enumerate((bp, bm, b1, b2)):
-            nc.scalar.dma_start(bias_rows[i * CB : (i + 1) * CB, :], vec.rearrange("(a p) o -> a (p o)", p=P))
+            nc.scalar.dma_start(bias_rows[i * CB : (i + 1) * CB, :], vec.rearrange("(b p) o -> b (p o)", p=P))
         ident_f = held.tile([BIAS_ROWS, BIAS_ROWS], F32, name="ident_f")
         make_identity(nc, ident_f[:])
-        bias_ps = psum_tr.tile([P, BANK], F32, name="bias_ps", tag="tr")
+        bias_ps = psum_t.tile([P, BANK], F32, name="bias_ps", tag="t")
         nc.tensor.transpose(bias_ps[:, 0:BIAS_ROWS], bias_rows[:], ident_f[:])
         bias_cols = held.tile([P, 4 * CB], F32, name="bias_cols")
         nc.vector.tensor_copy(bias_cols[:], bias_ps[:, 0 : 4 * CB])
-        bias_t = {name: bias_cols[:, i * CB : (i + 1) * CB] for i, name in enumerate(("bp", "bm", "b1", "b2"))}
+        bp_t, bm_t, b1_t, b2_t = [bias_cols[:, i * CB : (i + 1) * CB] for i in range(4)]
 
         with tc.tile_pool(name="table", bufs=1) as table:
             emb_t = [table.tile([P, S], F32, name=f"emb{c}") for c in range(CB)]
             pos_t = [table.tile([P, N], F32, name=f"pos{c}") for c in range(CB)]
             for c in range(CB):
                 if c == CB - 1:
-                    nc.sync.dma_start(wp_t[:], wp.rearrange("(a p) d -> p a d", p=P))
+                    nc.sync.dma_start(wp_t[:], wp.rearrange("(b p) d -> p b d", p=P))
                 nc.sync.dma_start(emb_t[c][:], embed[blk(c), :])
                 nc.sync.dma_start(pos_t[c][:], pos[blk(c), :])
-            nc.sync.dma_start(wm_t[:], wm.rearrange("(a p) d -> p a d", p=P))
-            nc.sync.dma_start(w1_t[:], w1.rearrange("(a p) d -> p a d", p=P))
-            nc.sync.dma_start(w2_t[:], w2.rearrange("(a p) d -> p a d", p=P))
+            nc.sync.dma_start(wm_t[:], wm.rearrange("(b p) d -> p b d", p=P))
+            nc.sync.dma_start(w1_t[:], w1.rearrange("(b p) d -> p b d", p=P))
+            nc.sync.dma_start(w2_t[:], w2.rearrange("(b p) d -> p b d", p=P))
 
-            lenders = [(psum_s, "s")] * 5 + [(psum_mm, "mm")] * 2 + [(psum_tr, "tr")]
-            p_ps = [
-                [lenders[hf * CB + d][0].tile([P, BANK], F32, name=f"p_ps{d}_{hf}", tag=lenders[hf * CB + d][1]) for hf in range(NH)]
-                for d in range(CB)
-            ]
+            def borrowed_bank(i, name):
+                if i < S_BANKS:
+                    return psum_s.tile([P, BANK], F32, name=name, tag="s")
+                if i < S_BANKS + Y_BANKS:
+                    return psum_y.tile([P, BANK], F32, name=name, tag="y")
+                return psum_t.tile([P, BANK], F32, name=name, tag="t")
+
+            p_ps = [[borrowed_bank(hf * CB + d, f"p_ps{d}_{hf}") for hf in range(NH)] for d in range(CB)]
             for c in range(CB):
                 for hf in range(NH):
                     picked = emb_t[c][:].indirect(offsets[:, hf * (BANK // 16) : (hf + 1) * (BANK // 16)])
@@ -108,19 +119,14 @@ def tile_trm_b_kernel(tc, embed, pos, wp, bp, wm, bm, w1, b1, w2, b2, offs, out)
                     nc.scalar.copy(h_bf[c][:, half(hf)], h[c][:, half(hf)])
                     for d in range(CB):
                         nc.tensor.matmul(
-                            p_ps[d][hf][:], wp_t[:, c, blk(d)], h_bf[c][:, half(hf)],
-                            start=(c == 0), stop=(c == CB - 1),
+                            p_ps[d][hf][:], wp_t[:, c, blk(d)], h_bf[c][:, half(hf)], start=(c == 0), stop=(c == CB - 1)
                         )
             for hf in range(NH):
                 for d in range(CB):
                     if d % 2 == 0:
-                        nc.scalar.activation(
-                            p_bf[d][:, half(hf)], p_ps[d][hf][:], FUNC.Identity, bias=bias_t["bp"][:, d : d + 1]
-                        )
+                        nc.scalar.activation(p_bf[d][:, half(hf)], p_ps[d][hf][:], FUNC.Identity, bias=bp_t[:, d : d + 1])
                     else:
-                        nc.vector.tensor_scalar(
-                            p_bf[d][:, half(hf)], p_ps[d][hf][:], bias_t["bp"][:, d : d + 1], None, op0=ADD
-                        )
+                        nc.vector.tensor_scalar(p_bf[d][:, half(hf)], p_ps[d][hf][:], bp_t[:, d : d + 1], None, op0=ADD)
 
         with (
             tc.tile_pool(name="acts", bufs=1) as acts,
@@ -135,25 +141,22 @@ def tile_trm_b_kernel(tc, embed, pos, wp, bp, wm, bm, w1, b1, w2, b2, offs, out)
                 nc.gpsimd.tensor_tensor(wms[:, d, :], pair01[:, d, :], pair23[:, d, :], ADD)
 
             def whole_array_norm(stats, tag):
-                tot = psum_tr.tile([P, BANK], F32, name="tot", tag="tr")
-                k = stats.shape[2]
-                nc.tensor.matmul(tot[:, 0 : 2 * k], mean_w[:], stats[:].rearrange("p s k -> p (s k)"), start=True, stop=True)
+                tot = psum_t.tile([P, BANK], F32, name="tot", tag="t")
+                nc.tensor.matmul(tot[:, 0 : 2 * GROUPS], mean_w[:], stats[:].rearrange("p s g -> p (s g)"), start=True, stop=True)
                 mom = small.tile([P, 2], F32, name="mom" + tag)
-                nc.vector.tensor_reduce(mom[:], tot[:, 0 : 2 * k].rearrange("p (s k) -> p s k", s=2), axis=X, op=ADD)
-                negvar = small.tile([P, 1], F32, name="negvar" + tag)
-                nc.vector.tensor_scalar(negvar[:], mom[:, 0:1], mom[:, 0:1], mom[:, 1:2], op0=MULT, op1=ADD)
+                nc.vector.tensor_reduce(mom[:], tot[:, 0 : 2 * GROUPS].rearrange("p (s g) -> p s g", s=2), axis=X, op=ADD)
+                neg_var = small.tile([P, 1], F32, name="neg_var" + tag)
+                nc.vector.tensor_scalar(neg_var[:], mom[:, 0:1], mom[:, 0:1], mom[:, 1:2], op0=MULT, op1=ADD)
                 sigma = small.tile([P, 1], F32, name="sigma" + tag)
-                nc.scalar.activation(sigma[:], negvar[:], FUNC.Sqrt, bias=eps_t[:], scale=-1.0)
-                rstd = small.tile([P, 1], F32, name="rstd" + tag)
-                nc.vector.reciprocal(rstd[:], sigma[:])
+                nc.scalar.activation(sigma[:], neg_var[:], FUNC.Sqrt, bias=eps_t[:], scale=-1.0)
+                rho = small.tile([P, 1], F32, name="rho" + tag)
+                nc.vector.reciprocal(rho[:], sigma[:])
                 shift = small.tile([P, 1], F32, name="shift" + tag)
-                nc.vector.tensor_scalar(shift[:], mom[:, 0:1], rstd[:], None, op0=MULT)
-                return mom[:, 0:1], sigma, rstd, shift
+                nc.vector.tensor_scalar(shift[:], mom[:, 0:1], rho[:], None, op0=MULT)
+                return {"neg_mean": mom[:, 0:1], "sigma": sigma[:], "rho": rho[:], "shift": shift[:]}
 
-            vT = [acts.tile([P, C], BF16, name=f"vT{t}") for t in range(NB)]
+            vT = [acts.tile([P, C], BF16, name=f"vT{tb}") for tb in range(NB)]
             aT = [acts.tile([P, NB, BANK], BF16, name=f"aT{hf}") for hf in range(NH)]
-            y = [acts.tile([P, N], F32, name=f"y{c}") for c in range(CB)]
-            y_stats = acts.tile([P, 2, CB * NH], F32, name="y_stats")
 
             e_of, sums_of, a_of = {}, {}, {}
 
@@ -186,13 +189,13 @@ def tile_trm_b_kernel(tc, embed, pos, wp, bp, wm, bm, w1, b1, w2, b2, offs, out)
                 nc.scalar.activation(a_of[jb][:], e_of[jb][:], FUNC.Identity, scale=inv[:])
 
             def transpose_weights(jb):
-                a_tr = psum_tr.tile([P, N], BF16, name="a_tr", tag="tr")
+                a_tr = psum_t.tile([P, N], BF16, name="a_tr", tag="t")
                 for tb in range(NB):
                     nc.tensor.transpose(a_tr[:, blk(tb)], a_of[jb][:, blk(tb)], ident[:])
                 nc.vector.tensor_copy(aT[jb // JB][:, :, blk(jb % JB)], a_tr[:].rearrange("p (t j) -> p t j", t=NB))
 
             def v_block(tb):
-                v_ps = psum_mm.tile([P, BANK], F32, name="v_ps", tag="mm")
+                v_ps = psum_s.tile([P, BANK], F32, name="v_ps", tag="s")
                 for d in range(CB):
                     nc.tensor.matmul(v_ps[:], p_bf[d][:, blk(tb)], wms[:, d, :], start=(d == 0), stop=(d == CB - 1))
                 if tb % 2 == 0:
@@ -200,108 +203,107 @@ def tile_trm_b_kernel(tc, embed, pos, wp, bp, wm, bm, w1, b1, w2, b2, offs, out)
                 else:
                     nc.vector.tensor_copy(vT[tb][:], v_ps[:])
 
-            for step in range(NB + 2):
+            for step in range(NB + LAG_C):
                 if step < NB:
                     scores_and_exp(step)
                 else:
-                    v_block(2 * (step - NB))
-                    v_block(2 * (step - NB) + 1)
-                if 1 <= step <= NB:
-                    normalise(step - 1)
-                if step >= 2:
-                    transpose_weights(step - 2)
-            for tb in range(4, NB):
+                    for i in range(V_IN_DRAIN):
+                        v_block((step - NB) * V_IN_DRAIN + i)
+                if LAG_B <= step < NB + LAG_B:
+                    normalise(step - LAG_B)
+                if step >= LAG_C:
+                    transpose_weights(step - LAG_C)
+            for tb in range(LAG_C * V_IN_DRAIN, NB):
                 v_block(tb)
 
-            cs_ps = psum_tr.tile([P, BANK], F32, name="cs_ps", tag="tr")
+            colsum_ps = psum_t.tile([P, BANK], F32, name="colsum_ps", tag="t")
             for d in range(CB):
                 for c in range(CB):
-                    nc.tensor.matmul(cs_ps[:, d : d + 1], w1_t[:, c, blk(d)], ones_bf[:], start=(c == 0), stop=(c == CB - 1))
+                    nc.tensor.matmul(colsum_ps[:, d : d + 1], w1_t[:, c, blk(d)], ones_bf[:], start=(c == 0), stop=(c == CB - 1))
             w1_colsum = acts.tile([P, CB], F32, name="w1_colsum")
-            nc.vector.tensor_copy(w1_colsum[:], cs_ps[:, 0:CB])
+            nc.vector.tensor_copy(w1_colsum[:], colsum_ps[:, 0:CB])
 
+            y = [acts.tile([P, N], F32, name=f"y{c}") for c in range(CB)]
+            y_stats = acts.tile([P, 2, GROUPS], F32, name="y_stats")
             yc_bf = [acts.tile([P, N], BF16, name=f"yc_bf{c}") for c in range(CB)]
             neg_m0 = acts.tile([P, 1], F32, name="neg_m0")
 
             def centre(hf, c):
                 nc.gpsimd.tensor_scalar(yc_bf[c][:, half(hf)], y[c][:, half(hf)], 1.0, neg_m0[:], op0=MULT, op1=ADD)
 
-            for k in range(NH * CB):
-                hf, c = divmod(k, CB)
-                y_ps = psum_mm.tile([P, BANK], F32, name="y_ps", tag="mm")
+            for g in range(GROUPS):
+                hf, c = divmod(g, CB)
+                y_ps = psum_y.tile([P, BANK], F32, name="y_ps", tag="y")
                 for tb in range(NB):
                     nc.tensor.matmul(y_ps[:], vT[tb][:, blk(c)], aT[hf][:, tb, :], start=(tb == 0), stop=(tb == NB - 1))
-                if k == CB:
-                    m0_ps = psum_tr.tile([P, BANK], F32, name="m0_ps", tag="tr")
+                if g == CB:
+                    m0_ps = psum_t.tile([P, BANK], F32, name="m0_ps", tag="t")
                     nc.tensor.matmul(m0_ps[:, 0:CB], half_mean_w[:], y_stats[:, 0, 0:CB], start=True, stop=True)
                     nc.vector.tensor_reduce(neg_m0[:], m0_ps[:, 0:CB], axis=X, op=ADD)
                     for c0 in range(CB):
                         centre(0, c0)
                 nc.vector.scalar_tensor_tensor(
-                    y[c][:, half(hf)], y_ps[:], bias_t["bm"][:, c : c + 1], h[c][:, half(hf)], op0=ADD, op1=ADD,
-                    accum_out=y_stats[:, 0, k : k + 1],
+                    y[c][:, half(hf)], y_ps[:], bm_t[:, c : c + 1], h[c][:, half(hf)], op0=ADD, op1=ADD,
+                    accum_out=y_stats[:, 0, g : g + 1],
                 )
-                sq = work.tile([P, BANK], BF16, name="sq")
-                nc.scalar.activation(sq[:], y[c][:, half(hf)], FUNC.Square, accum_out=y_stats[:, 1, k : k + 1])
+                y_sq = work.tile([P, BANK], BF16, name="y_sq")
+                nc.scalar.activation(y_sq[:], y[c][:, half(hf)], FUNC.Square, accum_out=y_stats[:, 1, g : g + 1])
                 if hf == 1:
                     centre(1, c)
 
-            f_bf = [acts.tile([P, N], BF16, name=f"f_bf{d}") for d in range(CB)]
-
-            def f_products(k):
-                hf, d = divmod(k, CB)
+            def w1_products(g):
+                hf, d = divmod(g, CB)
                 f_ps = psum_s.tile([P, BANK], F32, name="f_ps", tag="s")
                 for c in range(CB):
                     nc.tensor.matmul(f_ps[:], w1_t[:, c, blk(d)], yc_bf[c][:, half(hf)], start=(c == 0), stop=(c == CB - 1))
                 return f_ps
 
-            AHEAD = 2
-            f_early = [f_products(k) for k in range(AHEAD)]
+            f_early = [w1_products(g) for g in range(AHEAD)]
 
-            neg_mean1, sigma1, rstd1, shift1 = whole_array_norm(y_stats, "1")
+            norm1 = whole_array_norm(y_stats, "1")
             drift = small.tile([P, 1], F32, name="drift")
-            nc.vector.tensor_scalar(drift[:], neg_mean1, neg_m0[:], None, op0=SUB)
-            drift_cs = small.tile([P, CB], F32, name="drift_cs")
-            nc.vector.tensor_scalar(drift_cs[:], w1_colsum[:], drift[:], None, op0=MULT)
+            nc.vector.tensor_scalar(drift[:], norm1["neg_mean"], neg_m0[:], None, op0=SUB)
+            drift_colsum = small.tile([P, CB], F32, name="drift_colsum")
+            nc.vector.tensor_scalar(drift_colsum[:], w1_colsum[:], drift[:], None, op0=MULT)
             f_bias = small.tile([P, CB], F32, name="f_bias")
-            nc.vector.scalar_tensor_tensor(f_bias[:], bias_t["b1"], sigma1[:], drift_cs[:], op0=MULT, op1=ADD)
+            nc.vector.scalar_tensor_tensor(f_bias[:], b1_t, norm1["sigma"], drift_colsum[:], op0=MULT, op1=ADD)
             shift_b2 = small.tile([P, CB], F32, name="shift_b2")
-            nc.vector.tensor_scalar(shift_b2[:], bias_t["b2"], shift1[:], None, op0=ADD)
+            nc.vector.tensor_scalar(shift_b2[:], b2_t, norm1["shift"], None, op0=ADD)
 
-            for k in range(NH * CB):
-                hf, d = divmod(k, CB)
-                f_ps = f_early[k] if k < AHEAD else f_products(k)
+            sf_bf = [acts.tile([P, N], BF16, name=f"sf_bf{d}") for d in range(CB)]
+            for g in range(GROUPS):
+                hf, d = divmod(g, CB)
+                f_ps = f_early[g] if g < AHEAD else w1_products(g)
                 if d % 2 == 0:
-                    nc.scalar.activation(f_bf[d][:, half(hf)], f_ps[:], FUNC.Relu, bias=f_bias[:, d : d + 1])
+                    nc.scalar.activation(sf_bf[d][:, half(hf)], f_ps[:], FUNC.Relu, bias=f_bias[:, d : d + 1])
                 else:
-                    nc.vector.tensor_scalar(f_bf[d][:, half(hf)], f_ps[:], f_bias[:, d : d + 1], 0.0, op0=ADD, op1=MAX)
+                    nc.vector.tensor_scalar(sf_bf[d][:, half(hf)], f_ps[:], f_bias[:, d : d + 1], 0.0, op0=ADD, op1=MAX)
 
             h1_b2 = [acts.tile([P, N], F32, name=f"h1_b2_{c}") for c in range(CB)]
             for c in range(CB):
-                nc.gpsimd.tensor_scalar(h1_b2[c][:], y[c][:], rstd1[:], shift_b2[:, c : c + 1], op0=MULT, op1=ADD)
+                nc.gpsimd.tensor_scalar(h1_b2[c][:], y[c][:], norm1["rho"], shift_b2[:, c : c + 1], op0=MULT, op1=ADD)
 
             z = [acts.tile([P, N], F32, name=f"z{c}") for c in range(CB)]
-            z_stats = acts.tile([P, 2, CB * NH], F32, name="z_stats")
-            for k in range(NH * CB):
-                hf, c = divmod(k, CB)
-                z_ps = psum_mm.tile([P, BANK], F32, name="z_ps", tag="mm")
+            z_stats = acts.tile([P, 2, GROUPS], F32, name="z_stats")
+            for g in range(GROUPS):
+                hf, c = divmod(g, CB)
+                z_ps = psum_s.tile([P, BANK], F32, name="z_ps", tag="s")
                 for d in range(CB):
-                    nc.tensor.matmul(z_ps[:], w2_t[:, d, blk(c)], f_bf[d][:, half(hf)], start=(d == 0), stop=(d == CB - 1))
+                    nc.tensor.matmul(z_ps[:], w2_t[:, d, blk(c)], sf_bf[d][:, half(hf)], start=(d == 0), stop=(d == CB - 1))
                 nc.vector.scalar_tensor_tensor(
-                    z[c][:, half(hf)], z_ps[:], rstd1[:], h1_b2[c][:, half(hf)], op0=MULT, op1=ADD,
-                    accum_out=z_stats[:, 0, k : k + 1],
+                    z[c][:, half(hf)], z_ps[:], norm1["rho"], h1_b2[c][:, half(hf)], op0=MULT, op1=ADD,
+                    accum_out=z_stats[:, 0, g : g + 1],
                 )
-                sq = work.tile([P, BANK], BF16, name="sq")
-                nc.scalar.activation(sq[:], z[c][:, half(hf)], FUNC.Square, accum_out=z_stats[:, 1, k : k + 1])
+                z_sq = work.tile([P, BANK], BF16, name="z_sq")
+                nc.scalar.activation(z_sq[:], z[c][:, half(hf)], FUNC.Square, accum_out=z_stats[:, 1, g : g + 1])
 
-            neg_mean2, sigma2, rstd2, shift2 = whole_array_norm(z_stats, "2")
-
+            norm2 = whole_array_norm(z_stats, "2")
             res = [acts.tile([P, N], F32, name=f"res{c}") for c in range(CB)]
             for c in range(CB):
                 for hf in range(NH):
                     if (c * NH + hf) % 3 < 2:
-                        nc.vector.tensor_scalar(res[c][:, half(hf)], z[c][:, half(hf)], neg_mean2, rstd2[:], op0=ADD, op1=MULT)
+                        nc.vector.tensor_scalar(res[c][:, half(hf)], z[c][:, half(hf)], norm2["neg_mean"], norm2["rho"], op0=ADD, op1=MULT)
                         nc.sync.dma_start(out[blk(c), half(hf)], res[c][:, half(hf)])
                     else:
-                        nc.scalar.activation(res[c][:, half(hf)], z[c][:, half(hf)], FUNC.Identity, bias=shift2[:], scale=rstd2[:])
+                        nc.scalar.activation(res[c][:, half(hf)], z[c][:, half(hf)], FUNC.Identity, bias=norm2["shift"], scale=norm2["rho"])
                         nc.scalar.dma_start(out[blk(c), half(hf)], res[c][:, half(hf)])

@@ -33,7 +33,7 @@ T_BANKS = 1
 
 BIAS_ROWS = 64
 LAG_B = 1
-LAG_C = 2
+LAG_C = 3
 V_IN_DRAIN = 2
 AHEAD = 2
 

@@ -35,6 +35,7 @@ BIAS_ROWS = 64
 LAG_B = 1
 LAG_C = 3
 V_IN_DRAIN = 2
+V_FROM = 8
 AHEAD = 2
 
 FLOPS = 2 * (4 * C * C * N + 2 * N * N * C)
@@ -84,10 +85,10 @@ def tile_trm_b_kernel(tc, embed, pos, wp, bp, wm, bm, w1, b1, w2, b2, offs, out)
         nc.vector.memset(bias_rows[:], 0.0)
         for i, vec in enumerate((bp, bm, b1, b2)):
             nc.scalar.dma_start(bias_rows[i * CB : (i + 1) * CB, :], vec.rearrange("(b p) o -> b (p o)", p=P))
-        ident_f = held.tile([BIAS_ROWS, BIAS_ROWS], F32, name="ident_f")
+        ident_f = held.tile([P, P], F32, name="ident_f")
         make_identity(nc, ident_f[:])
         bias_ps = psum_t.tile([P, BANK], F32, name="bias_ps", tag="t")
-        nc.tensor.transpose(bias_ps[:, 0:BIAS_ROWS], bias_rows[:], ident_f[:])
+        nc.tensor.transpose(bias_ps[:, 0:BIAS_ROWS], bias_rows[:], ident_f[0:BIAS_ROWS, 0:BIAS_ROWS])
         bias_cols = held.tile([P, 4 * CB], F32, name="bias_cols")
         nc.vector.tensor_copy(bias_cols[:], bias_ps[:, 0 : 4 * CB])
         bp_t, bm_t, b1_t, b2_t = [bias_cols[:, i * CB : (i + 1) * CB] for i in range(4)]
@@ -160,16 +161,25 @@ def tile_trm_b_kernel(tc, embed, pos, wp, bp, wm, bm, w1, b1, w2, b2, offs, out)
 
             e_of, sums_of, a_of = {}, {}, {}
 
+            kept = [acts.tile([P, BANK], F32, name=f"kept{jb}") for jb in range(JB)]
+
             def scores_and_exp(jb):
                 s_ps = [psum_s.tile([P, BANK], F32, name=f"s_ps{hf}", tag="s") for hf in range(NH)]
                 for hf in range(NH):
-                    for d in range(CB):
-                        nc.tensor.matmul(
-                            s_ps[hf][:], p_bf[d][:, blk(jb)], p_bf[d][:, half(hf)], start=(d == 0), stop=(d == CB - 1)
-                        )
+                    if hf == 0 and jb >= JB:
+                        for tb in range(JB):
+                            nc.tensor.transpose(s_ps[0][:, blk(tb)], kept[tb][:, blk(jb - JB)], ident_f[:])
+                    else:
+                        for d in range(CB):
+                            nc.tensor.matmul(
+                                s_ps[hf][:], p_bf[d][:, blk(jb)], p_bf[d][:, half(hf)], start=(d == 0), stop=(d == CB - 1)
+                            )
                 tops = small.tile([P, NH], F32, name="tops")
                 for hf in range(NH):
-                    nc.vector.tensor_reduce(tops[:, hf : hf + 1], s_ps[hf][:], axis=X, op=MAX)
+                    if hf == 1 and jb < JB:
+                        nc.vector.tensor_scalar(kept[jb][:], s_ps[1][:], 1.0, None, op0=MULT, op1=MAX, accum_out=tops[:, 1:2])
+                    else:
+                        nc.vector.tensor_reduce(tops[:, hf : hf + 1], s_ps[hf][:], axis=X, op=MAX)
                 neg_top = small.tile([P, 1], F32, name="neg_top")
                 nc.vector.tensor_scalar(neg_top[:], tops[:, 0:1], tops[:, 1:2], -SCALE, op0=MAX, op1=MULT)
                 e_of[jb] = work.tile([P, N], F32, name="e")
@@ -186,7 +196,10 @@ def tile_trm_b_kernel(tc, embed, pos, wp, bp, wm, bm, w1, b1, w2, b2, offs, out)
                 inv = small.tile([P, 1], F32, name="inv")
                 nc.vector.reciprocal(inv[:], total[:])
                 a_of[jb] = work.tile([P, N], BF16, name="a")
-                nc.scalar.activation(a_of[jb][:], e_of[jb][:], FUNC.Identity, scale=inv[:])
+                if jb < JB:
+                    nc.scalar.activation(a_of[jb][:], e_of[jb][:], FUNC.Identity, scale=inv[:])
+                else:
+                    nc.gpsimd.tensor_scalar(a_of[jb][:], e_of[jb][:], inv[:], 0.0, op0=MULT, op1=ADD)
 
             def transpose_weights(jb):
                 a_tr = psum_t.tile([P, N], BF16, name="a_tr", tag="t")
@@ -203,17 +216,18 @@ def tile_trm_b_kernel(tc, embed, pos, wp, bp, wm, bm, w1, b1, w2, b2, offs, out)
                 else:
                     nc.vector.tensor_copy(vT[tb][:], v_ps[:])
 
+            v_left = list(range(NB))
             for step in range(NB + LAG_C):
                 if step < NB:
                     scores_and_exp(step)
-                else:
-                    for i in range(V_IN_DRAIN):
-                        v_block((step - NB) * V_IN_DRAIN + i)
+                for tb in v_left[: (0 if step < V_FROM else 1 if step < NB else V_IN_DRAIN)]:
+                    v_block(tb)
+                    v_left.remove(tb)
                 if LAG_B <= step < NB + LAG_B:
                     normalise(step - LAG_B)
                 if step >= LAG_C:
                     transpose_weights(step - LAG_C)
-            for tb in range(LAG_C * V_IN_DRAIN, NB):
+            for tb in v_left:
                 v_block(tb)
 
             colsum_ps = psum_t.tile([P, BANK], F32, name="colsum_ps", tag="t")

@@ -141,17 +141,17 @@ def tile_trm_b_kernel(tc, embed, pos, wp, bp, wm, bm, w1, b1, w2, b2, offs, out)
                 nc.gpsimd.tensor_tensor(pair23[:, d, :], wm_t[:, 2 * CB + d, :], wm_t[:, 3 * CB + d, :], ADD)
                 nc.gpsimd.tensor_tensor(wms[:, d, :], pair01[:, d, :], pair23[:, d, :], ADD)
 
-            def whole_array_norm(stats, tag):
+            def whole_array_norm(stats, pieces, tag):
                 tot = psum_t.tile([P, BANK], F32, name="tot", tag="t")
-                nc.tensor.matmul(tot[:, 0 : 2 * GROUPS], mean_w[:], stats[:].rearrange("p s g -> p (s g)"), start=True, stop=True)
+                nc.tensor.matmul(tot[:, 0 : 2 * pieces], mean_w[:], stats[:].rearrange("p s g -> p (s g)"), start=True, stop=True)
                 mom = small.tile([P, 2], F32, name="mom" + tag)
-                nc.vector.tensor_reduce(mom[:], tot[:, 0 : 2 * GROUPS].rearrange("p (s g) -> p s g", s=2), axis=X, op=ADD)
+                nc.vector.tensor_reduce(mom[:], tot[:, 0 : 2 * pieces].rearrange("p (s g) -> p s g", s=2), axis=X, op=ADD)
                 neg_var = small.tile([P, 1], F32, name="neg_var" + tag)
                 nc.vector.tensor_scalar(neg_var[:], mom[:, 0:1], mom[:, 0:1], mom[:, 1:2], op0=MULT, op1=ADD)
-                sigma = small.tile([P, 1], F32, name="sigma" + tag)
-                nc.scalar.activation(sigma[:], neg_var[:], FUNC.Sqrt, bias=eps_t[:], scale=-1.0)
                 rho = small.tile([P, 1], F32, name="rho" + tag)
-                nc.vector.reciprocal(rho[:], sigma[:])
+                nc.scalar.activation(rho[:], neg_var[:], FUNC.Abs_reciprocal_sqrt, bias=eps_t[:], scale=-1.0)
+                sigma = small.tile([P, 1], F32, name="sigma" + tag)
+                nc.vector.reciprocal(sigma[:], rho[:])
                 shift = small.tile([P, 1], F32, name="shift" + tag)
                 nc.vector.tensor_scalar(shift[:], mom[:, 0:1], rho[:], None, op0=MULT)
                 return {"neg_mean": mom[:, 0:1], "sigma": sigma[:], "rho": rho[:], "shift": shift[:]}
@@ -274,7 +274,7 @@ def tile_trm_b_kernel(tc, embed, pos, wp, bp, wm, bm, w1, b1, w2, b2, offs, out)
 
             f_early = [w1_products(g) for g in range(AHEAD)]
 
-            norm1 = whole_array_norm(y_stats, "1")
+            norm1 = whole_array_norm(y_stats, GROUPS, "1")
             drift = small.tile([P, 1], F32, name="drift")
             nc.vector.tensor_scalar(drift[:], norm1["neg_mean"], neg_m0[:], None, op0=SUB)
             drift_colsum = small.tile([P, CB], F32, name="drift_colsum")
@@ -298,20 +298,22 @@ def tile_trm_b_kernel(tc, embed, pos, wp, bp, wm, bm, w1, b1, w2, b2, offs, out)
                 nc.gpsimd.tensor_scalar(h1_b2[c][:], y[c][:], norm1["rho"], shift_b2[:, c : c + 1], op0=MULT, op1=ADD)
 
             z = [acts.tile([P, N], F32, name=f"z{c}") for c in range(CB)]
-            z_stats = acts.tile([P, 2, GROUPS], F32, name="z_stats")
-            for g in range(GROUPS):
-                hf, c = divmod(g, CB)
+            z_pieces = [(g % CB, (g // CB) * BANK, BANK) for g in range(GROUPS - 1)]
+            z_pieces += [(CB - 1, N - BANK + i * (BANK // 2), BANK // 2) for i in range(2)]
+            z_stats = acts.tile([P, 2, len(z_pieces)], F32, name="z_stats")
+            for i, (c, t0, width) in enumerate(z_pieces):
+                cols = slice(t0, t0 + width)
                 z_ps = psum_s.tile([P, BANK], F32, name="z_ps", tag="s")
                 for d in range(CB):
-                    nc.tensor.matmul(z_ps[:], w2_t[:, d, blk(c)], sf_bf[d][:, half(hf)], start=(d == 0), stop=(d == CB - 1))
+                    nc.tensor.matmul(z_ps[:, 0:width], w2_t[:, d, blk(c)], sf_bf[d][:, cols], start=(d == 0), stop=(d == CB - 1))
                 nc.vector.scalar_tensor_tensor(
-                    z[c][:, half(hf)], z_ps[:], norm1["rho"], h1_b2[c][:, half(hf)], op0=MULT, op1=ADD,
-                    accum_out=z_stats[:, 0, g : g + 1],
+                    z[c][:, cols], z_ps[:, 0:width], norm1["rho"], h1_b2[c][:, cols], op0=MULT, op1=ADD,
+                    accum_out=z_stats[:, 0, i : i + 1],
                 )
                 z_sq = work.tile([P, BANK], BF16, name="z_sq")
-                nc.scalar.activation(z_sq[:], z[c][:, half(hf)], FUNC.Square, accum_out=z_stats[:, 1, g : g + 1])
+                nc.scalar.activation(z_sq[:, 0:width], z[c][:, cols], FUNC.Square, accum_out=z_stats[:, 1, i : i + 1])
 
-            norm2 = whole_array_norm(z_stats, "2")
+            norm2 = whole_array_norm(z_stats, len(z_pieces), "2")
             res = [acts.tile([P, N], F32, name=f"res{c}") for c in range(CB)]
             for c in range(CB):
                 for hf in range(NH):

@@ -97,10 +97,15 @@ def tile_trm_b_kernel(tc, embed, pos, wp, bp, wm, bm, w1, b1, w2, b2, offs, out)
             emb_t = [table.tile([P, S], F32, name=f"emb{c}") for c in range(CB)]
             pos_t = [table.tile([P, N], F32, name=f"pos{c}") for c in range(CB)]
             for c in range(CB):
-                if c == CB - 1:
-                    nc.sync.dma_start(wp_t[:], wp.rearrange("(b p) d -> p b d", p=P))
                 nc.sync.dma_start(emb_t[c][:], embed[blk(c), :])
-                nc.sync.dma_start(pos_t[c][:], pos[blk(c), :])
+                if c == CB - 2:
+                    nc.sync.dma_start(wp_t[:, 0 : CB - 1, :], wp[0 : (CB - 1) * P, :].rearrange("(b p) d -> p b d", p=P))
+                if c < CB - 1:
+                    nc.sync.dma_start(pos_t[c][:], pos[blk(c), :])
+                else:
+                    for hf in range(NH):
+                        nc.sync.dma_start(pos_t[c][:, half(hf)], pos[blk(c), half(hf)])
+                    nc.sync.dma_start(wp_t[:, c, :], wp[blk(c), :])
             nc.sync.dma_start(wm_t[:], wm.rearrange("(b p) d -> p b d", p=P))
             nc.sync.dma_start(w1_t[:], w1.rearrange("(b p) d -> p b d", p=P))
             nc.sync.dma_start(w2_t[:], w2.rearrange("(b p) d -> p b d", p=P))
@@ -136,10 +141,9 @@ def tile_trm_b_kernel(tc, embed, pos, wp, bp, wm, bm, w1, b1, w2, b2, offs, out)
             pair01 = acts.tile([P, CB, C], F32, name="pair01")
             pair23 = acts.tile([P, CB, C], F32, name="pair23")
             wms = acts.tile([P, CB, C], BF16, name="wms")
-            for d in range(CB):
-                nc.gpsimd.tensor_tensor(pair01[:, d, :], wm_t[:, d, :], wm_t[:, CB + d, :], ADD)
-                nc.gpsimd.tensor_tensor(pair23[:, d, :], wm_t[:, 2 * CB + d, :], wm_t[:, 3 * CB + d, :], ADD)
-                nc.gpsimd.tensor_tensor(wms[:, d, :], pair01[:, d, :], pair23[:, d, :], ADD)
+            nc.gpsimd.tensor_tensor(pair01[:], wm_t[:, 0:CB, :], wm_t[:, CB : 2 * CB, :], ADD)
+            nc.gpsimd.tensor_tensor(pair23[:], wm_t[:, 2 * CB : 3 * CB, :], wm_t[:, 3 * CB : 4 * CB, :], ADD)
+            nc.gpsimd.tensor_tensor(wms[:], pair01[:], pair23[:], ADD)
 
             def whole_array_norm(stats, pieces, tag):
                 tot = psum_t.tile([P, BANK], F32, name="tot", tag="t")

@@ -97,14 +97,17 @@ def tile_trm_b_kernel(tc, embed, pos, wp, bp, wm, bm, w1, b1, w2, b2, offs, out)
             emb_t = [table.tile([P, S], F32, name=f"emb{c}") for c in range(CB)]
             pos_t = [table.tile([P, N], F32, name=f"pos{c}") for c in range(CB)]
             for c in range(CB):
-                nc.sync.dma_start(emb_t[c][:], embed[blk(c), :])
                 if c == CB - 2:
+                    nc.sync.dma_start(emb_t[c][:, 0 : S // 2], embed[blk(c), 0 : S // 2])
                     nc.sync.dma_start(wp_t[:, 0 : CB - 1, :], wp[0 : (CB - 1) * P, :].rearrange("(b p) d -> p b d", p=P))
+                    nc.sync.dma_start(emb_t[c][:, S // 2 : S], embed[blk(c), S // 2 : S])
+                else:
+                    nc.sync.dma_start(emb_t[c][:], embed[blk(c), :])
                 if c < CB - 1:
                     nc.sync.dma_start(pos_t[c][:], pos[blk(c), :])
                 else:
-                    for hf in range(NH):
-                        nc.sync.dma_start(pos_t[c][:, half(hf)], pos[blk(c), half(hf)])
+                    for t0 in range(0, N, BANK // 2):
+                        nc.sync.dma_start(pos_t[c][:, t0 : t0 + BANK // 2], pos[blk(c), t0 : t0 + BANK // 2])
                     nc.sync.dma_start(wp_t[:, c, :], wp[blk(c), :])
             nc.sync.dma_start(wm_t[:], wm.rearrange("(b p) d -> p b d", p=P))
             nc.sync.dma_start(w1_t[:], w1.rearrange("(b p) d -> p b d", p=P))
@@ -119,13 +122,17 @@ def tile_trm_b_kernel(tc, embed, pos, wp, bp, wm, bm, w1, b1, w2, b2, offs, out)
 
             p_ps = [[borrowed_bank(hf * CB + d, f"p_ps{d}_{hf}") for hf in range(NH)] for d in range(CB)]
             for c in range(CB):
-                for hf in range(NH):
-                    picked = emb_t[c][:].indirect(offsets[:, hf * (BANK // 16) : (hf + 1) * (BANK // 16)])
-                    nc.vector.tensor_tensor(h[c][:, half(hf)], picked, pos_t[c][:, half(hf)], ADD)
-                    nc.scalar.copy(h_bf[c][:, half(hf)], h[c][:, half(hf)])
+                width = BANK // 2 if c == CB - 1 else BANK
+                for t0 in range(0, N, width):
+                    cols = slice(t0, t0 + width)
+                    picked = emb_t[c][:].indirect(offsets[:, t0 // 16 : (t0 + width) // 16])
+                    nc.vector.tensor_tensor(h[c][:, cols], picked, pos_t[c][:, cols], ADD)
+                    nc.scalar.copy(h_bf[c][:, cols], h[c][:, cols])
+                    hf, b0 = divmod(t0, BANK)
                     for d in range(CB):
                         nc.tensor.matmul(
-                            p_ps[d][hf][:], wp_t[:, c, blk(d)], h_bf[c][:, half(hf)], start=(c == 0), stop=(c == CB - 1)
+                            p_ps[d][hf][:, b0 : b0 + width], wp_t[:, c, blk(d)], h_bf[c][:, cols],
+                            start=(c == 0), stop=(c == CB - 1 and b0 + width == BANK),
                         )
             for hf in range(NH):
                 for d in range(CB):

@@ -109,7 +109,10 @@ def tile_trm_b_kernel(tc, embed, pos, wp, bp, wm, bm, w1, b1, w2, b2, offs, out)
                     for t0 in range(0, N, BANK // 2):
                         nc.sync.dma_start(pos_t[c][:, t0 : t0 + BANK // 2], pos[blk(c), t0 : t0 + BANK // 2])
                     nc.sync.dma_start(wp_t[:, c, :], wp[blk(c), :])
-            nc.sync.dma_start(wm_t[:], wm.rearrange("(b p) d -> p b d", p=P))
+            for i in range(2):
+                nc.sync.dma_start(
+                    wm_t[:, 2 * i * CB : 2 * (i + 1) * CB, :], wm[2 * i * C : 2 * (i + 1) * C, :].rearrange("(b p) d -> p b d", p=P)
+                )
             nc.sync.dma_start(w1_t[:], w1.rearrange("(b p) d -> p b d", p=P))
             nc.sync.dma_start(w2_t[:], w2.rearrange("(b p) d -> p b d", p=P))
 

@@ -27,15 +27,10 @@ GROUPS = NH * CB
 EPS = 1e-5
 SCALE = 1.0 / math.sqrt(C)
 
-S_BANKS = 5
-Y_BANKS = 2
+S_BANKS = 7
 T_BANKS = 1
 
 BIAS_ROWS = 64
-LAG_B = 1
-LAG_C = 3
-V_IN_DRAIN = 2
-V_FROM = 8
 AHEAD = 2
 
 FLOPS = 2 * (4 * C * C * N + 2 * N * N * C)
@@ -54,7 +49,6 @@ def tile_trm_b_kernel(tc, embed, pos, wp, bp, wm, bm, w1, b1, w2, b2, offs, out)
         tc.tile_pool(name="held", bufs=1) as held,
         tc.tile_pool(name="small", bufs=4) as small,
         tc.psum_pool(name="psum_s", bufs=S_BANKS) as psum_s,
-        tc.psum_pool(name="psum_y", bufs=Y_BANKS) as psum_y,
         tc.psum_pool(name="psum_t", bufs=T_BANKS) as psum_t,
     ):
         offsets = held.tile([P, N // 16], U16, name="offsets")
@@ -74,7 +68,7 @@ def tile_trm_b_kernel(tc, embed, pos, wp, bp, wm, bm, w1, b1, w2, b2, offs, out)
         nc.vector.memset(mean_w[:], -1.0 / (C * N))
         half_mean_w = held.tile([P, P], F32, name="half_mean_w")
         nc.vector.memset(half_mean_w[:], -1.0 / (C * BANK))
-        ones_bf = held.tile([P, 1], BF16, name="ones_bf")
+        ones_bf = held.tile([P, P], BF16, name="ones_bf")
         nc.vector.memset(ones_bf[:], 1.0)
         eps_t = held.tile([P, 1], F32, name="eps_t")
         nc.vector.memset(eps_t[:], EPS)
@@ -119,8 +113,6 @@ def tile_trm_b_kernel(tc, embed, pos, wp, bp, wm, bm, w1, b1, w2, b2, offs, out)
             def borrowed_bank(i, name):
                 if i < S_BANKS:
                     return psum_s.tile([P, BANK], F32, name=name, tag="s")
-                if i < S_BANKS + Y_BANKS:
-                    return psum_y.tile([P, BANK], F32, name=name, tag="y")
                 return psum_t.tile([P, BANK], F32, name=name, tag="t")
 
             p_ps = [[borrowed_bank(hf * CB + d, f"p_ps{d}_{hf}") for hf in range(NH)] for d in range(CB)]
@@ -154,6 +146,10 @@ def tile_trm_b_kernel(tc, embed, pos, wp, bp, wm, bm, w1, b1, w2, b2, offs, out)
             nc.gpsimd.tensor_tensor(pair01[:], wm_t[:, 0:CB, :], wm_t[:, CB : 2 * CB, :], ADD)
             nc.gpsimd.tensor_tensor(pair23[:], wm_t[:, 2 * CB : 3 * CB, :], wm_t[:, 3 * CB : 4 * CB, :], ADD)
             nc.gpsimd.tensor_tensor(wms[:], pair01[:], pair23[:], ADD)
+            w1_pairs = acts.tile([P, CB // 2, C], F32, name="w1_pairs")
+            w1_sum = acts.tile([P, C], BF16, name="w1_sum")
+            nc.gpsimd.tensor_tensor(w1_pairs[:], w1_t[:, 0 : CB // 2, :], w1_t[:, CB // 2 : CB, :], ADD)
+            nc.gpsimd.tensor_tensor(w1_sum[:], w1_pairs[:, 0, :], w1_pairs[:, 1, :], ADD)
 
             def whole_array_norm(stats, pieces, tag):
                 tot = psum_t.tile([P, BANK], F32, name="tot", tag="t")
@@ -173,29 +169,24 @@ def tile_trm_b_kernel(tc, embed, pos, wp, bp, wm, bm, w1, b1, w2, b2, offs, out)
             vT = [acts.tile([P, C], BF16, name=f"vT{tb}") for tb in range(NB)]
             aT = [acts.tile([P, NB, BANK], BF16, name=f"aT{hf}") for hf in range(NH)]
 
-            e_of, sums_of, a_of = {}, {}, {}
-
-            kept = [acts.tile([P, BANK], F32, name=f"kept{jb}") for jb in range(JB)]
+            kept = [acts.tile([P, BANK], F32, name=f"kept{tb}") for tb in range(NB)]
+            top_late = acts.tile([P, JB], F32, name="top_late")
+            e_of, sums_of, a_of, col_top_of = {}, {}, {}, {}
 
             def scores_and_exp(jb):
                 s_ps = [psum_s.tile([P, BANK], F32, name=f"s_ps{hf}", tag="s") for hf in range(NH)]
                 for hf in range(NH):
-                    if hf == 0 and jb >= JB:
-                        for tb in range(JB):
-                            nc.tensor.transpose(s_ps[0][:, blk(tb)], kept[tb][:, blk(jb - JB)], ident_f[:])
-                    else:
-                        for d in range(CB):
-                            nc.tensor.matmul(
-                                s_ps[hf][:], p_bf[d][:, blk(jb)], p_bf[d][:, half(hf)], start=(d == 0), stop=(d == CB - 1)
-                            )
+                    for d in range(CB):
+                        nc.tensor.matmul(s_ps[hf][:], p_bf[d][:, blk(jb)], p_bf[d][:, half(hf)], start=(d == 0), stop=(d == CB - 1))
                 tops = small.tile([P, NH], F32, name="tops")
-                for hf in range(NH):
-                    if hf == 1 and jb < JB:
-                        nc.vector.tensor_scalar(kept[jb][:], s_ps[1][:], 1.0, None, op0=MULT, op1=MAX, accum_out=tops[:, 1:2])
-                    else:
-                        nc.vector.tensor_reduce(tops[:, hf : hf + 1], s_ps[hf][:], axis=X, op=MAX)
+                nc.vector.tensor_reduce(tops[:, 0:1], s_ps[0][:], axis=X, op=MAX)
+                nc.vector.tensor_scalar(kept[jb][:], s_ps[1][:], 1.0, None, op0=MULT, op1=MAX, accum_out=tops[:, 1:2])
                 neg_top = small.tile([P, 1], F32, name="neg_top")
                 nc.vector.tensor_scalar(neg_top[:], tops[:, 0:1], tops[:, 1:2], -SCALE, op0=MAX, op1=MULT)
+                if jb > 0:
+                    col_top_of[jb] = work.tile([P, BANK], F32, name="col_top", tag="col")
+                    before = kept[0] if jb == 1 else col_top_of[jb - 1]
+                    nc.vector.tensor_tensor(col_top_of[jb][:], s_ps[1][:], before[:], MAX)
                 e_of[jb] = work.tile([P, N], F32, name="e")
                 sums_of[jb] = small.tile([P, NH], F32, name="sums")
                 for hf in range(NH):
@@ -209,17 +200,31 @@ def tile_trm_b_kernel(tc, embed, pos, wp, bp, wm, bm, w1, b1, w2, b2, offs, out)
                 nc.vector.tensor_reduce(total[:], sums_of[jb][:], axis=X, op=ADD)
                 inv = small.tile([P, 1], F32, name="inv")
                 nc.vector.reciprocal(inv[:], total[:])
-                a_of[jb] = work.tile([P, N], BF16, name="a")
-                if jb < JB:
-                    nc.scalar.activation(a_of[jb][:], e_of[jb][:], FUNC.Identity, scale=inv[:])
-                else:
-                    nc.gpsimd.tensor_scalar(a_of[jb][:], e_of[jb][:], inv[:], 0.0, op0=MULT, op1=ADD)
+                a_of[jb] = acts.tile([P, N], BF16, name=f"a{jb}")
+                nc.scalar.activation(a_of[jb][:], e_of[jb][:], FUNC.Identity, scale=inv[:])
 
             def transpose_weights(jb):
                 a_tr = psum_t.tile([P, N], BF16, name="a_tr", tag="t")
                 for tb in range(NB):
                     nc.tensor.transpose(a_tr[:, blk(tb)], a_of[jb][:, blk(tb)], ident[:])
-                nc.vector.tensor_copy(aT[jb // JB][:, :, blk(jb % JB)], a_tr[:].rearrange("p (t j) -> p t j", t=NB))
+                nc.vector.tensor_copy(aT[0][:, :, blk(jb)], a_tr[:].rearrange("p (t j) -> p t j", t=NB))
+
+            def scores_kept(tb):
+                s_ps = psum_s.tile([P, BANK], F32, name="s_ps", tag="s")
+                for d in range(CB):
+                    nc.tensor.matmul(s_ps[:], p_bf[d][:, blk(tb)], p_bf[d][:, half(1)], start=(d == 0), stop=(d == CB - 1))
+                nc.vector.tensor_scalar(
+                    kept[tb][:], s_ps[:], 1.0, None, op0=MULT, op1=MAX, accum_out=top_late[:, tb - JB : tb - JB + 1]
+                )
+
+            def spread(bank, column):
+                for b in range(JB):
+                    nc.tensor.transpose(bank[:, blk(b)], column[:, b : b + 1].to_broadcast([P, P]), ident_f[:])
+
+            def exp_kept(tb):
+                diff = work.tile([P, BANK], F32, name="diff", tag="bank")
+                nc.vector.tensor_tensor(diff[:], kept[tb][:], neg_tops_ps[:], ADD)
+                nc.scalar.activation(aT[1][:, tb, :], diff[:], FUNC.Exp, scale=SCALE)
 
             def v_block(tb):
                 v_ps = psum_s.tile([P, BANK], F32, name="v_ps", tag="s")
@@ -230,24 +235,46 @@ def tile_trm_b_kernel(tc, embed, pos, wp, bp, wm, bm, w1, b1, w2, b2, offs, out)
                 else:
                     nc.vector.tensor_copy(vT[tb][:], v_ps[:])
 
-            v_left = list(range(NB))
-            for step in range(NB + LAG_C):
-                if step < NB:
-                    scores_and_exp(step)
-                for tb in v_left[: (0 if step < V_FROM else 1 if step < NB else V_IN_DRAIN)]:
-                    v_block(tb)
-                    v_left.remove(tb)
-                if LAG_B <= step < NB + LAG_B:
-                    normalise(step - LAG_B)
-                if step >= LAG_C:
-                    transpose_weights(step - LAG_C)
-            for tb in v_left:
-                v_block(tb)
+            for step in range(JB):
+                scores_and_exp(step)
+                if step >= 1:
+                    normalise(step - 1)
+            for step in range(JB):
+                scores_kept(JB + step)
+                if step == 0:
+                    normalise(JB - 1)
+                if step == JB - 2:
+                    col_ps = psum_s.tile([P, BANK], F32, name="col_ps", tag="s")
+                    for b in range(JB):
+                        nc.tensor.transpose(col_ps[:, blk(b)], col_top_of[JB - 1][:, blk(b)], ident_f[:])
+                    top_early = acts.tile([P, JB], F32, name="top_early")
+                    nc.vector.tensor_reduce(top_early[:], col_ps[:].rearrange("p (b t) -> p b t", b=JB), axis=X, op=MAX)
+                transpose_weights(step)
+            neg_tops = acts.tile([P, JB], F32, name="neg_tops")
+            for b in range(JB):
+                nc.vector.tensor_scalar(
+                    neg_tops[:, b : b + 1], top_early[:, b : b + 1], top_late[:, b : b + 1], -1.0, op0=MAX, op1=MULT
+                )
+            v_block(0)
+            neg_tops_ps = psum_s.tile([P, BANK], F32, name="neg_tops_ps", tag="s")
+            spread(neg_tops_ps, neg_tops)
+            e_sum = None
+            for tb in range(NB):
+                if tb < NB - 1:
+                    v_block(tb + 1)
+                exp_kept(tb)
+                if tb > 0:
+                    before = aT[1][:, 0, :] if tb == 1 else e_sum[:]
+                    e_sum = work.tile([P, BANK], F32, name="e_sum", tag="col")
+                    nc.gpsimd.tensor_tensor(e_sum[:], before, aT[1][:, tb, :], ADD)
+            e_sum_hi = acts.tile([P, BANK], BF16, name="e_sum_hi")
+            e_sum_lo = acts.tile([P, BANK], BF16, name="e_sum_lo")
+            nc.gpsimd.tensor_copy(e_sum_hi[:], e_sum[:])
+            nc.gpsimd.tensor_tensor(e_sum_lo[:], e_sum[:], e_sum_hi[:], SUB)
 
             colsum_ps = psum_t.tile([P, BANK], F32, name="colsum_ps", tag="t")
             for d in range(CB):
-                for c in range(CB):
-                    nc.tensor.matmul(colsum_ps[:, d : d + 1], w1_t[:, c, blk(d)], ones_bf[:], start=(c == 0), stop=(c == CB - 1))
+                nc.tensor.matmul(colsum_ps[:, d : d + 1], w1_sum[:, blk(d)], ones_bf[:, 0:1], start=True, stop=True)
             w1_colsum = acts.tile([P, CB], F32, name="w1_colsum")
             nc.vector.tensor_copy(w1_colsum[:], colsum_ps[:, 0:CB])
 
@@ -256,12 +283,16 @@ def tile_trm_b_kernel(tc, embed, pos, wp, bp, wm, bm, w1, b1, w2, b2, offs, out)
             yc_bf = [acts.tile([P, N], BF16, name=f"yc_bf{c}") for c in range(CB)]
             neg_m0 = acts.tile([P, 1], F32, name="neg_m0")
 
-            def centre(hf, c):
-                nc.gpsimd.tensor_scalar(yc_bf[c][:, half(hf)], y[c][:, half(hf)], 1.0, neg_m0[:], op0=MULT, op1=ADD)
-
+            inv_b = acts.tile([P, BANK], F32, name="inv_b")
             for g in range(GROUPS):
                 hf, c = divmod(g, CB)
-                y_ps = psum_y.tile([P, BANK], F32, name="y_ps", tag="y")
+                if g == CB:
+                    sum_ps = psum_t.tile([P, BANK], F32, name="sum_ps", tag="t")
+                    nc.tensor.matmul(sum_ps[:], ones_bf[:], e_sum_hi[:], start=True, stop=False)
+                    nc.tensor.matmul(sum_ps[:], ones_bf[:], e_sum_lo[:], start=False, stop=True)
+                    nc.scalar.activation(inv_b[:], sum_ps[:], FUNC.Abs_reciprocal_sqrt)
+                    nc.scalar.activation(inv_b[:], inv_b[:], FUNC.Square)
+                y_ps = psum_s.tile([P, BANK], F32, name="y_ps", tag="s")
                 for tb in range(NB):
                     nc.tensor.matmul(y_ps[:], vT[tb][:, blk(c)], aT[hf][:, tb, :], start=(tb == 0), stop=(tb == NB - 1))
                 if g == CB:
@@ -269,15 +300,20 @@ def tile_trm_b_kernel(tc, embed, pos, wp, bp, wm, bm, w1, b1, w2, b2, offs, out)
                     nc.tensor.matmul(m0_ps[:, 0:CB], half_mean_w[:], y_stats[:, 0, 0:CB], start=True, stop=True)
                     nc.vector.tensor_reduce(neg_m0[:], m0_ps[:, 0:CB], axis=X, op=ADD)
                     for c0 in range(CB):
-                        centre(0, c0)
+                        nc.gpsimd.tensor_scalar(yc_bf[c0][:, half(0)], y[c0][:, half(0)], 1.0, neg_m0[:], op0=MULT, op1=ADD)
+                if hf == 0:
+                    y_in = y_ps
+                else:
+                    y_in = work.tile([P, BANK], F32, name="y_in", tag="bank")
+                    nc.vector.tensor_tensor(y_in[:], y_ps[:], inv_b[:], MULT)
                 nc.vector.scalar_tensor_tensor(
-                    y[c][:, half(hf)], y_ps[:], bm_t[:, c : c + 1], h[c][:, half(hf)], op0=ADD, op1=ADD,
+                    y[c][:, half(hf)], y_in[:], bm_t[:, c : c + 1], h[c][:, half(hf)], op0=ADD, op1=ADD,
                     accum_out=y_stats[:, 0, g : g + 1],
                 )
                 y_sq = work.tile([P, BANK], BF16, name="y_sq")
                 nc.scalar.activation(y_sq[:], y[c][:, half(hf)], FUNC.Square, accum_out=y_stats[:, 1, g : g + 1])
                 if hf == 1:
-                    centre(1, c)
+                    nc.scalar.activation(yc_bf[c][:, half(1)], y[c][:, half(1)], FUNC.Identity, bias=neg_m0[:])
 
             def w1_products(g):
                 hf, d = divmod(g, CB)
@@ -328,7 +364,7 @@ def tile_trm_b_kernel(tc, embed, pos, wp, bp, wm, bm, w1, b1, w2, b2, offs, out)
                 nc.scalar.activation(z_sq[:, 0:width], z[c][:, cols], FUNC.Square, accum_out=z_stats[:, 1, i : i + 1])
 
             norm2 = whole_array_norm(z_stats, len(z_pieces), "2")
-            res = [acts.tile([P, N], F32, name=f"res{c}") for c in range(CB)]
+            res = [acts.tile([P, N], F32, name=f"res{c}", tag=f"y{c}") for c in range(CB)]
             for c in range(CB):
                 for hf in range(NH):
                     if (c * NH + hf) % 3 < 2:

@@ -141,14 +141,14 @@ def tile_trm_b_kernel(tc, embed, pos, wp, bp, wm, bm, w1, b1, w2, b2, offs, out)
             tc.tile_pool(name="work", bufs=3) as work,
         ):
             pair01 = acts.tile([P, CB, C], F32, name="pair01")
-            pair23 = acts.tile([P, CB, C], F32, name="pair23")
+            pair23 = acts.tile([P, CB, C], F32, name="pair23", tag="pair")
             wms = acts.tile([P, CB, C], BF16, name="wms")
             nc.gpsimd.tensor_tensor(pair01[:], wm_t[:, 0:CB, :], wm_t[:, CB : 2 * CB, :], ADD)
             nc.gpsimd.tensor_tensor(pair23[:], wm_t[:, 2 * CB : 3 * CB, :], wm_t[:, 3 * CB : 4 * CB, :], ADD)
             nc.gpsimd.tensor_tensor(wms[:], pair01[:], pair23[:], ADD)
-            w1_pairs = acts.tile([P, CB // 2, C], F32, name="w1_pairs")
+            w1_pairs = acts.tile([P, CB, C], F32, name="w1_pairs", tag="pair")
             w1_sum = acts.tile([P, C], BF16, name="w1_sum")
-            nc.gpsimd.tensor_tensor(w1_pairs[:], w1_t[:, 0 : CB // 2, :], w1_t[:, CB // 2 : CB, :], ADD)
+            nc.gpsimd.tensor_tensor(w1_pairs[:, 0 : CB // 2, :], w1_t[:, 0 : CB // 2, :], w1_t[:, CB // 2 : CB, :], ADD)
             nc.gpsimd.tensor_tensor(w1_sum[:], w1_pairs[:, 0, :], w1_pairs[:, 1, :], ADD)
 
             def whole_array_norm(stats, pieces, tag):
@@ -211,10 +211,15 @@ def tile_trm_b_kernel(tc, embed, pos, wp, bp, wm, bm, w1, b1, w2, b2, offs, out)
 
             def scores_kept(tb):
                 s_ps = psum_s.tile([P, BANK], F32, name="s_ps", tag="s")
+                b = tb - JB
                 for d in range(CB):
-                    nc.tensor.matmul(s_ps[:], p_bf[d][:, blk(tb)], p_bf[d][:, half(1)], start=(d == 0), stop=(d == CB - 1))
+                    nc.tensor.matmul(
+                        s_ps[:, b * P : BANK], p_bf[d][:, blk(tb)], p_bf[d][:, tb * P : N], start=(d == 0), stop=(d == CB - 1)
+                    )
+                for i in range(b):
+                    nc.tensor.transpose(s_ps[:, blk(i)], kept[JB + i][:, blk(b)], ident_f[:])
                 nc.vector.tensor_scalar(
-                    kept[tb][:], s_ps[:], 1.0, None, op0=MULT, op1=MAX, accum_out=top_late[:, tb - JB : tb - JB + 1]
+                    kept[tb][:], s_ps[:], 1.0, None, op0=MULT, op1=MAX, accum_out=top_late[:, b : b + 1]
                 )
 
             def spread(bank, column):
@@ -287,7 +292,7 @@ def tile_trm_b_kernel(tc, embed, pos, wp, bp, wm, bm, w1, b1, w2, b2, offs, out)
             for g in range(GROUPS):
                 hf, c = divmod(g, CB)
                 if g == CB:
-                    sum_ps = psum_t.tile([P, BANK], F32, name="sum_ps", tag="t")
+                    sum_ps = psum_s.tile([P, BANK], F32, name="sum_ps", tag="s")
                     nc.tensor.matmul(sum_ps[:], ones_bf[:], e_sum_hi[:], start=True, stop=False)
                     nc.tensor.matmul(sum_ps[:], ones_bf[:], e_sum_lo[:], start=False, stop=True)
                     nc.scalar.activation(inv_b[:], sum_ps[:], FUNC.Abs_reciprocal_sqrt)

@@ -31,6 +31,7 @@ S_BANKS = 7
 T_BANKS = 1
 
 BIAS_ROWS = 64
+V_OPEN = 4
 AHEAD = 2
 
 FLOPS = 2 * (4 * C * C * N + 2 * N * N * C)
@@ -143,9 +144,12 @@ def tile_trm_b_kernel(tc, embed, pos, wp, bp, wm, bm, w1, b1, w2, b2, offs, out)
             pair01 = acts.tile([P, CB, C], F32, name="pair01")
             pair23 = acts.tile([P, CB, C], F32, name="pair23", tag="pair")
             wms = acts.tile([P, CB, C], BF16, name="wms")
-            nc.gpsimd.tensor_tensor(pair01[:], wm_t[:, 0:CB, :], wm_t[:, CB : 2 * CB, :], ADD)
-            nc.gpsimd.tensor_tensor(pair23[:], wm_t[:, 2 * CB : 3 * CB, :], wm_t[:, 3 * CB : 4 * CB, :], ADD)
-            nc.gpsimd.tensor_tensor(wms[:], pair01[:], pair23[:], ADD)
+            for d0 in range(0, CB, CB // 2):
+                part = [slice(k * CB + d0, k * CB + d0 + CB // 2) for k in range(HEADS)]
+                ds = part[0]
+                nc.gpsimd.tensor_tensor(pair01[:, ds, :], wm_t[:, part[0], :], wm_t[:, part[1], :], ADD)
+                nc.gpsimd.tensor_tensor(pair23[:, ds, :], wm_t[:, part[2], :], wm_t[:, part[3], :], ADD)
+                nc.gpsimd.tensor_tensor(wms[:, ds, :], pair01[:, ds, :], pair23[:, ds, :], ADD)
             w1_pairs = acts.tile([P, CB, C], F32, name="w1_pairs", tag="pair")
             w1_sum = acts.tile([P, C], BF16, name="w1_sum")
             nc.gpsimd.tensor_tensor(w1_pairs[:, 0 : CB // 2, :], w1_t[:, 0 : CB // 2, :], w1_t[:, CB // 2 : CB, :], ADD)
@@ -169,24 +173,29 @@ def tile_trm_b_kernel(tc, embed, pos, wp, bp, wm, bm, w1, b1, w2, b2, offs, out)
             vT = [acts.tile([P, C], BF16, name=f"vT{tb}") for tb in range(NB)]
             aT = [acts.tile([P, NB, BANK], BF16, name=f"aT{hf}") for hf in range(NH)]
 
-            kept = [acts.tile([P, BANK], F32, name=f"kept{tb}") for tb in range(NB)]
+            kept = acts.tile([P, NB, BANK], F32, name="kept")
             top_late = acts.tile([P, JB], F32, name="top_late")
-            e_of, sums_of, a_of, col_top_of = {}, {}, {}, {}
+            e_of, sums_of, a_of = {}, {}, {}
+
+            square = [acts.tile([P, BANK], F32, name=f"square{jb}") for jb in range(JB)]
+
+            def products(bank, row_block, first, cols):
+                for d in range(CB):
+                    nc.tensor.matmul(
+                        bank[:, first * P : BANK], p_bf[d][:, blk(row_block)], p_bf[d][:, cols], start=(d == 0), stop=(d == CB - 1)
+                    )
 
             def scores_and_exp(jb):
                 s_ps = [psum_s.tile([P, BANK], F32, name=f"s_ps{hf}", tag="s") for hf in range(NH)]
-                for hf in range(NH):
-                    for d in range(CB):
-                        nc.tensor.matmul(s_ps[hf][:], p_bf[d][:, blk(jb)], p_bf[d][:, half(hf)], start=(d == 0), stop=(d == CB - 1))
                 tops = small.tile([P, NH], F32, name="tops")
-                nc.vector.tensor_reduce(tops[:, 0:1], s_ps[0][:], axis=X, op=MAX)
-                nc.vector.tensor_scalar(kept[jb][:], s_ps[1][:], 1.0, None, op0=MULT, op1=MAX, accum_out=tops[:, 1:2])
+                products(s_ps[0], jb, jb, slice(jb * P, BANK))
+                products(s_ps[1], jb, 0, half(1))
+                for i in range(jb):
+                    nc.tensor.transpose(s_ps[0][:, blk(i)], square[i][:, blk(jb)], ident_f[:])
+                nc.vector.tensor_scalar(square[jb][:], s_ps[0][:], 1.0, None, op0=MULT, op1=MAX, accum_out=tops[:, 0:1])
+                nc.vector.tensor_scalar(kept[:, jb, :], s_ps[1][:], 1.0, None, op0=MULT, op1=MAX, accum_out=tops[:, 1:2])
                 neg_top = small.tile([P, 1], F32, name="neg_top")
                 nc.vector.tensor_scalar(neg_top[:], tops[:, 0:1], tops[:, 1:2], -SCALE, op0=MAX, op1=MULT)
-                if jb > 0:
-                    col_top_of[jb] = work.tile([P, BANK], F32, name="col_top", tag="col")
-                    before = kept[0] if jb == 1 else col_top_of[jb - 1]
-                    nc.vector.tensor_tensor(col_top_of[jb][:], s_ps[1][:], before[:], MAX)
                 e_of[jb] = work.tile([P, N], F32, name="e")
                 sums_of[jb] = small.tile([P, NH], F32, name="sums")
                 for hf in range(NH):
@@ -207,19 +216,17 @@ def tile_trm_b_kernel(tc, embed, pos, wp, bp, wm, bm, w1, b1, w2, b2, offs, out)
                 a_tr = psum_t.tile([P, N], BF16, name="a_tr", tag="t")
                 for tb in range(NB):
                     nc.tensor.transpose(a_tr[:, blk(tb)], a_of[jb][:, blk(tb)], ident[:])
-                nc.vector.tensor_copy(aT[0][:, :, blk(jb)], a_tr[:].rearrange("p (t j) -> p t j", t=NB))
+                copy_out = nc.scalar.copy if jb % 2 == 0 else nc.vector.tensor_copy
+                copy_out(aT[0][:, :, blk(jb)], a_tr[:].rearrange("p (t j) -> p t j", t=NB))
 
             def scores_kept(tb):
                 s_ps = psum_s.tile([P, BANK], F32, name="s_ps", tag="s")
                 b = tb - JB
-                for d in range(CB):
-                    nc.tensor.matmul(
-                        s_ps[:, b * P : BANK], p_bf[d][:, blk(tb)], p_bf[d][:, tb * P : N], start=(d == 0), stop=(d == CB - 1)
-                    )
+                products(s_ps, tb, b, slice(tb * P, N))
                 for i in range(b):
-                    nc.tensor.transpose(s_ps[:, blk(i)], kept[JB + i][:, blk(b)], ident_f[:])
+                    nc.tensor.transpose(s_ps[:, blk(i)], kept[:, JB + i, blk(b)], ident_f[:])
                 nc.vector.tensor_scalar(
-                    kept[tb][:], s_ps[:], 1.0, None, op0=MULT, op1=MAX, accum_out=top_late[:, b : b + 1]
+                    kept[:, tb, :], s_ps[:], 1.0, None, op0=MULT, op1=MAX, accum_out=top_late[:, b : b + 1]
                 )
 
             def spread(bank, column):
@@ -228,17 +235,18 @@ def tile_trm_b_kernel(tc, embed, pos, wp, bp, wm, bm, w1, b1, w2, b2, offs, out)
 
             def exp_kept(tb):
                 diff = work.tile([P, BANK], F32, name="diff", tag="bank")
-                nc.vector.tensor_tensor(diff[:], kept[tb][:], neg_tops_ps[:], ADD)
+                nc.vector.tensor_tensor(diff[:], kept[:, tb, :], neg_tops_ps[:], ADD)
                 nc.scalar.activation(aT[1][:, tb, :], diff[:], FUNC.Exp, scale=SCALE)
 
-            def v_block(tb):
-                v_ps = psum_s.tile([P, BANK], F32, name="v_ps", tag="s")
-                for d in range(CB):
-                    nc.tensor.matmul(v_ps[:], p_bf[d][:, blk(tb)], wms[:, d, :], start=(d == 0), stop=(d == CB - 1))
-                if tb % 2 == 0:
-                    nc.scalar.copy(vT[tb][:], v_ps[:])
-                else:
-                    nc.vector.tensor_copy(vT[tb][:], v_ps[:])
+            v_ps_of = {}
+
+            def v_products(tb, ds):
+                if ds[0] == 0:
+                    v_ps_of[tb] = psum_s.tile([P, BANK], F32, name="v_ps", tag="s")
+                for d in ds:
+                    nc.tensor.matmul(v_ps_of[tb][:], p_bf[d][:, blk(tb)], wms[:, d, :], start=(d == 0), stop=(d == CB - 1))
+                if ds[-1] == CB - 1:
+                    nc.scalar.copy(vT[tb][:], v_ps_of[tb][:])
 
             for step in range(JB):
                 scores_and_exp(step)
@@ -248,25 +256,29 @@ def tile_trm_b_kernel(tc, embed, pos, wp, bp, wm, bm, w1, b1, w2, b2, offs, out)
                 scores_kept(JB + step)
                 if step == 0:
                     normalise(JB - 1)
-                if step == JB - 2:
-                    col_ps = psum_s.tile([P, BANK], F32, name="col_ps", tag="s")
-                    for b in range(JB):
-                        nc.tensor.transpose(col_ps[:, blk(b)], col_top_of[JB - 1][:, blk(b)], ident_f[:])
-                    top_early = acts.tile([P, JB], F32, name="top_early")
-                    nc.vector.tensor_reduce(top_early[:], col_ps[:].rearrange("p (b t) -> p b t", b=JB), axis=X, op=MAX)
                 transpose_weights(step)
+            col_top = acts.tile([P, BANK], F32, name="col_top")
+            nc.vector.tensor_reduce(col_top[:], kept[:, 0:JB, :].rearrange("p t j -> p j t"), axis=X, op=MAX)
+            for tb in range(V_OPEN):
+                v_products(tb, range(0, CB // 2))
+            col_ps = psum_s.tile([P, BANK], F32, name="col_ps", tag="s")
+            for b in range(JB):
+                nc.tensor.transpose(col_ps[:, blk(b)], col_top[:, blk(b)], ident_f[:])
+            top_early = acts.tile([P, JB], F32, name="top_early")
+            nc.vector.tensor_reduce(top_early[:], col_ps[:].rearrange("p (b t) -> p b t", b=JB), axis=X, op=MAX)
             neg_tops = acts.tile([P, JB], F32, name="neg_tops")
             for b in range(JB):
                 nc.vector.tensor_scalar(
                     neg_tops[:, b : b + 1], top_early[:, b : b + 1], top_late[:, b : b + 1], -1.0, op0=MAX, op1=MULT
                 )
-            v_block(0)
+            for tb in range(V_OPEN):
+                v_products(tb, range(CB // 2, CB))
             neg_tops_ps = psum_s.tile([P, BANK], F32, name="neg_tops_ps", tag="s")
             spread(neg_tops_ps, neg_tops)
             e_sum = None
             for tb in range(NB):
-                if tb < NB - 1:
-                    v_block(tb + 1)
+                if tb < NB - V_OPEN:
+                    v_products(V_OPEN + tb, range(CB))
                 exp_kept(tb)
                 if tb > 0:
                     before = aT[1][:, 0, :] if tb == 1 else e_sum[:]
@@ -291,16 +303,15 @@ def tile_trm_b_kernel(tc, embed, pos, wp, bp, wm, bm, w1, b1, w2, b2, offs, out)
             inv_b = acts.tile([P, BANK], F32, name="inv_b")
             for g in range(GROUPS):
                 hf, c = divmod(g, CB)
+                y_ps = psum_s.tile([P, BANK], F32, name="y_ps", tag="s")
+                for tb in range(NB):
+                    nc.tensor.matmul(y_ps[:], vT[tb][:, blk(c)], aT[hf][:, tb, :], start=(tb == 0), stop=(tb == NB - 1))
                 if g == CB:
                     sum_ps = psum_s.tile([P, BANK], F32, name="sum_ps", tag="s")
                     nc.tensor.matmul(sum_ps[:], ones_bf[:], e_sum_hi[:], start=True, stop=False)
                     nc.tensor.matmul(sum_ps[:], ones_bf[:], e_sum_lo[:], start=False, stop=True)
                     nc.scalar.activation(inv_b[:], sum_ps[:], FUNC.Abs_reciprocal_sqrt)
                     nc.scalar.activation(inv_b[:], inv_b[:], FUNC.Square)
-                y_ps = psum_s.tile([P, BANK], F32, name="y_ps", tag="s")
-                for tb in range(NB):
-                    nc.tensor.matmul(y_ps[:], vT[tb][:, blk(c)], aT[hf][:, tb, :], start=(tb == 0), stop=(tb == NB - 1))
-                if g == CB:
                     m0_ps = psum_t.tile([P, BANK], F32, name="m0_ps", tag="t")
                     nc.tensor.matmul(m0_ps[:, 0:CB], half_mean_w[:], y_stats[:, 0, 0:CB], start=True, stop=True)
                     nc.vector.tensor_reduce(neg_m0[:], m0_ps[:, 0:CB], axis=X, op=ADD)
@@ -352,7 +363,7 @@ def tile_trm_b_kernel(tc, embed, pos, wp, bp, wm, bm, w1, b1, w2, b2, offs, out)
             for c in range(CB):
                 nc.gpsimd.tensor_scalar(h1_b2[c][:], y[c][:], norm1["rho"], shift_b2[:, c : c + 1], op0=MULT, op1=ADD)
 
-            z = [acts.tile([P, N], F32, name=f"z{c}") for c in range(CB)]
+            z = [held.tile([P, N], F32, name=f"z{c}", tag=f"h{c}") for c in range(CB)]
             z_pieces = [(g % CB, (g // CB) * BANK, BANK) for g in range(GROUPS - 1)]
             z_pieces += [(CB - 1, N - BANK + i * (BANK // 2), BANK // 2) for i in range(2)]
             z_stats = acts.tile([P, 2, len(z_pieces)], F32, name="z_stats")

@@ -164,11 +164,7 @@ def tile_trm_b_kernel(tc, embed, pos, wp, bp, wm, bm, w1, b1, w2, b2, offs, out)
                 nc.vector.tensor_scalar(neg_var[:], mom[:, 0:1], mom[:, 0:1], mom[:, 1:2], op0=MULT, op1=ADD)
                 rho = small.tile([P, 1], F32, name="rho" + tag)
                 nc.scalar.activation(rho[:], neg_var[:], FUNC.Abs_reciprocal_sqrt, bias=eps_t[:], scale=-1.0)
-                sigma = small.tile([P, 1], F32, name="sigma" + tag)
-                nc.vector.reciprocal(sigma[:], rho[:])
-                shift = small.tile([P, 1], F32, name="shift" + tag)
-                nc.vector.tensor_scalar(shift[:], mom[:, 0:1], rho[:], None, op0=MULT)
-                return {"neg_mean": mom[:, 0:1], "sigma": sigma[:], "rho": rho[:], "shift": shift[:]}
+                return mom[:, 0:1], rho[:]
 
             vT = [acts.tile([P, C], BF16, name=f"vT{tb}") for tb in range(NB)]
             aT = [acts.tile([P, NB, BANK], BF16, name=f"aT{hf}") for hf in range(NH)]
@@ -300,6 +296,9 @@ def tile_trm_b_kernel(tc, embed, pos, wp, bp, wm, bm, w1, b1, w2, b2, offs, out)
             yc_bf = [acts.tile([P, N], BF16, name=f"yc_bf{c}") for c in range(CB)]
             neg_m0 = acts.tile([P, 1], F32, name="neg_m0")
 
+            def centre(hf, c):
+                nc.scalar.activation(yc_bf[c][:, half(hf)], y[c][:, half(hf)], FUNC.Identity, bias=neg_m0[:])
+
             inv_b = acts.tile([P, BANK], F32, name="inv_b")
             for g in range(GROUPS):
                 hf, c = divmod(g, CB)
@@ -316,7 +315,7 @@ def tile_trm_b_kernel(tc, embed, pos, wp, bp, wm, bm, w1, b1, w2, b2, offs, out)
                     nc.tensor.matmul(m0_ps[:, 0:CB], half_mean_w[:], y_stats[:, 0, 0:CB], start=True, stop=True)
                     nc.vector.tensor_reduce(neg_m0[:], m0_ps[:, 0:CB], axis=X, op=ADD)
                     for c0 in range(CB):
-                        nc.gpsimd.tensor_scalar(yc_bf[c0][:, half(0)], y[c0][:, half(0)], 1.0, neg_m0[:], op0=MULT, op1=ADD)
+                        centre(0, c0)
                 if hf == 0:
                     y_in = y_ps
                 else:
@@ -329,7 +328,7 @@ def tile_trm_b_kernel(tc, embed, pos, wp, bp, wm, bm, w1, b1, w2, b2, offs, out)
                 y_sq = work.tile([P, BANK], BF16, name="y_sq")
                 nc.scalar.activation(y_sq[:], y[c][:, half(hf)], FUNC.Square, accum_out=y_stats[:, 1, g : g + 1])
                 if hf == 1:
-                    nc.scalar.activation(yc_bf[c][:, half(1)], y[c][:, half(1)], FUNC.Identity, bias=neg_m0[:])
+                    centre(1, c)
 
             def w1_products(g):
                 hf, d = divmod(g, CB)
@@ -340,15 +339,19 @@ def tile_trm_b_kernel(tc, embed, pos, wp, bp, wm, bm, w1, b1, w2, b2, offs, out)
 
             f_early = [w1_products(g) for g in range(AHEAD)]
 
-            norm1 = whole_array_norm(y_stats, GROUPS, "1")
+            neg_mean1, rho1 = whole_array_norm(y_stats, GROUPS, "1")
+            sigma = small.tile([P, 1], F32, name="sigma")
+            nc.vector.reciprocal(sigma[:], rho1)
+            shift = small.tile([P, 1], F32, name="shift")
+            nc.vector.tensor_scalar(shift[:], neg_mean1, rho1, None, op0=MULT)
             drift = small.tile([P, 1], F32, name="drift")
-            nc.vector.tensor_scalar(drift[:], norm1["neg_mean"], neg_m0[:], None, op0=SUB)
+            nc.vector.tensor_scalar(drift[:], neg_mean1, neg_m0[:], None, op0=SUB)
             drift_colsum = small.tile([P, CB], F32, name="drift_colsum")
             nc.vector.tensor_scalar(drift_colsum[:], w1_colsum[:], drift[:], None, op0=MULT)
             f_bias = small.tile([P, CB], F32, name="f_bias")
-            nc.vector.scalar_tensor_tensor(f_bias[:], b1_t, norm1["sigma"], drift_colsum[:], op0=MULT, op1=ADD)
+            nc.vector.scalar_tensor_tensor(f_bias[:], b1_t, sigma[:], drift_colsum[:], op0=MULT, op1=ADD)
             shift_b2 = small.tile([P, CB], F32, name="shift_b2")
-            nc.vector.tensor_scalar(shift_b2[:], b2_t, norm1["shift"], None, op0=ADD)
+            nc.vector.tensor_scalar(shift_b2[:], b2_t, shift[:], None, op0=ADD)
 
             sf_bf = [acts.tile([P, N], BF16, name=f"sf_bf{d}") for d in range(CB)]
             for g in range(GROUPS):
@@ -361,7 +364,7 @@ def tile_trm_b_kernel(tc, embed, pos, wp, bp, wm, bm, w1, b1, w2, b2, offs, out)
 
             h1_b2 = [acts.tile([P, N], F32, name=f"h1_b2_{c}") for c in range(CB)]
             for c in range(CB):
-                nc.gpsimd.tensor_scalar(h1_b2[c][:], y[c][:], norm1["rho"], shift_b2[:, c : c + 1], op0=MULT, op1=ADD)
+                nc.gpsimd.tensor_scalar(h1_b2[c][:], y[c][:], rho1, shift_b2[:, c : c + 1], op0=MULT, op1=ADD)
 
             z = [held.tile([P, N], F32, name=f"z{c}", tag=f"h{c}") for c in range(CB)]
             z_pieces = [(g % CB, (g // CB) * BANK, BANK) for g in range(GROUPS - 1)]
@@ -373,19 +376,17 @@ def tile_trm_b_kernel(tc, embed, pos, wp, bp, wm, bm, w1, b1, w2, b2, offs, out)
                 for d in range(CB):
                     nc.tensor.matmul(z_ps[:, 0:width], w2_t[:, d, blk(c)], sf_bf[d][:, cols], start=(d == 0), stop=(d == CB - 1))
                 nc.vector.scalar_tensor_tensor(
-                    z[c][:, cols], z_ps[:, 0:width], norm1["rho"], h1_b2[c][:, cols], op0=MULT, op1=ADD,
+                    z[c][:, cols], z_ps[:, 0:width], rho1, h1_b2[c][:, cols], op0=MULT, op1=ADD,
                     accum_out=z_stats[:, 0, i : i + 1],
                 )
                 z_sq = work.tile([P, BANK], BF16, name="z_sq")
                 nc.scalar.activation(z_sq[:, 0:width], z[c][:, cols], FUNC.Square, accum_out=z_stats[:, 1, i : i + 1])
 
-            norm2 = whole_array_norm(z_stats, len(z_pieces), "2")
+            neg_mean2, rho2 = whole_array_norm(z_stats, len(z_pieces), "2")
             res = [acts.tile([P, N], F32, name=f"res{c}", tag=f"y{c}") for c in range(CB)]
             for c in range(CB):
-                for hf in range(NH):
-                    if (c * NH + hf) % 3 < 2:
-                        nc.vector.tensor_scalar(res[c][:, half(hf)], z[c][:, half(hf)], norm2["neg_mean"], norm2["rho"], op0=ADD, op1=MULT)
-                        nc.sync.dma_start(out[blk(c), half(hf)], res[c][:, half(hf)])
-                    else:
-                        nc.scalar.activation(res[c][:, half(hf)], z[c][:, half(hf)], FUNC.Identity, bias=norm2["shift"], scale=norm2["rho"])
-                        nc.scalar.dma_start(out[blk(c), half(hf)], res[c][:, half(hf)])
+                width = BANK if c < CB // 2 else N
+                for t0 in range(0, N, width):
+                    cols = slice(t0, t0 + width)
+                    nc.vector.tensor_scalar(res[c][:, cols], z[c][:, cols], neg_mean2, rho2, op0=ADD, op1=MULT)
+                    nc.sync.dma_start(out[blk(c), cols], res[c][:, cols])

@@ -227,7 +227,7 @@ def tile_trm_b_kernel(tc, embed, pos, wp, bp, wm, bm, w1, b1, w2, b2, offs, out)
 
             def spread(bank, column):
                 for b in range(JB):
-                    nc.tensor.transpose(bank[:, blk(b)], column[:, b : b + 1].to_broadcast([P, P]), ident_f[:])
+                    nc.tensor.transpose(bank[:, blk(b)], column[:, b : b + 1].to_broadcast([P, P]), ident[:])
 
             def exp_kept(tb):
                 diff = work.tile([P, BANK], F32, name="diff", tag="bank")
@@ -253,23 +253,23 @@ def tile_trm_b_kernel(tc, embed, pos, wp, bp, wm, bm, w1, b1, w2, b2, offs, out)
                 if step == 0:
                     normalise(JB - 1)
                 transpose_weights(step)
-            col_top = acts.tile([P, BANK], F32, name="col_top")
+            col_top = acts.tile([P, BANK], BF16, name="col_top")
             nc.vector.tensor_reduce(col_top[:], kept[:, 0:JB, :].rearrange("p t j -> p j t"), axis=X, op=MAX)
             for tb in range(V_OPEN):
                 v_products(tb, range(0, CB // 2))
-            col_ps = psum_s.tile([P, BANK], F32, name="col_ps", tag="s")
+            col_ps = psum_s.tile([P, BANK], BF16, name="col_ps", tag="s")
             for b in range(JB):
-                nc.tensor.transpose(col_ps[:, blk(b)], col_top[:, blk(b)], ident_f[:])
+                nc.tensor.transpose(col_ps[:, blk(b)], col_top[:, blk(b)], ident[:])
             top_early = acts.tile([P, JB], F32, name="top_early")
             nc.vector.tensor_reduce(top_early[:], col_ps[:].rearrange("p (b t) -> p b t", b=JB), axis=X, op=MAX)
-            neg_tops = acts.tile([P, JB], F32, name="neg_tops")
+            neg_tops = acts.tile([P, JB], BF16, name="neg_tops")
             for b in range(JB):
                 nc.vector.tensor_scalar(
                     neg_tops[:, b : b + 1], top_early[:, b : b + 1], top_late[:, b : b + 1], -1.0, op0=MAX, op1=MULT
                 )
             for tb in range(V_OPEN):
                 v_products(tb, range(CB // 2, CB))
-            neg_tops_ps = psum_s.tile([P, BANK], F32, name="neg_tops_ps", tag="s")
+            neg_tops_ps = psum_s.tile([P, BANK], BF16, name="neg_tops_ps", tag="s")
             spread(neg_tops_ps, neg_tops)
             e_sum = None
             for tb in range(NB):

import math

import concourse.mybir as mybir
from concourse.masks import make_identity

F32 = mybir.dt.float32
BF16 = mybir.dt.bfloat16
U16 = mybir.dt.uint16
ADD = mybir.AluOpType.add
SUB = mybir.AluOpType.subtract
MULT = mybir.AluOpType.mult
MAX = mybir.AluOpType.max
FUNC = mybir.ActivationFunctionType
X = mybir.AxisListType.X

P = 128
C = 512
S = 4096
N = 1024
HEADS = 4
CB = C // P
NB = N // P
BANK = 512
NH = N // BANK
JB = BANK // P
GROUPS = NH * CB
EPS = 1e-5
SCALE = 1.0 / math.sqrt(C)

S_BANKS = 7
T_BANKS = 1

BIAS_ROWS = 64
V_OPEN = 4
AHEAD = 2

FLOPS = 2 * (4 * C * C * N + 2 * N * N * C)


def tile_trm_b_kernel(tc, embed, pos, wp, bp, wm, bm, w1, b1, w2, b2, offs, out):
    nc = tc.nc

    def blk(i):
        return slice(i * P, (i + 1) * P)

    def half(i):
        return slice(i * BANK, (i + 1) * BANK)

    with (
        tc.tile_pool(name="held", bufs=1) as held,
        tc.tile_pool(name="small", bufs=4) as small,
        tc.psum_pool(name="psum_s", bufs=S_BANKS) as psum_s,
        tc.psum_pool(name="psum_t", bufs=T_BANKS) as psum_t,
    ):
        offsets = held.tile([P, N // 16], U16, name="offsets")
        nc.sync.dma_start(offsets[:], offs)

        wp_t = held.tile([P, CB, C], BF16, name="wp_t")
        wm_t = held.tile([P, HEADS * CB, C], BF16, name="wm_t")
        w1_t = held.tile([P, CB, C], BF16, name="w1_t")
        w2_t = held.tile([P, CB, C], BF16, name="w2_t")
        h = [held.tile([P, N], F32, name=f"h{c}") for c in range(CB)]
        h_bf = [held.tile([P, N], BF16, name=f"h_bf{c}") for c in range(CB)]
        p_bf = [held.tile([P, N], BF16, name=f"p_bf{d}") for d in range(CB)]

        ident = held.tile([P, P], BF16, name="ident")
        make_identity(nc, ident[:])
        mean_w = held.tile([P, P], F32, name="mean_w")
        nc.vector.memset(mean_w[:], -1.0 / (C * N))
        half_mean_w = held.tile([P, P], F32, name="half_mean_w")
        nc.vector.memset(half_mean_w[:], -1.0 / (C * BANK))
        ones_bf = held.tile([P, P], BF16, name="ones_bf")
        nc.vector.memset(ones_bf[:], 1.0)
        eps_t = held.tile([P, 1], F32, name="eps_t")
        nc.vector.memset(eps_t[:], EPS)
        warm = held.tile([P, 1], F32, name="warm")
        nc.scalar.activation(warm[:], eps_t[:], FUNC.Exp)

        bias_rows = held.tile([BIAS_ROWS, P], F32, name="bias_rows")
        nc.vector.memset(bias_rows[:], 0.0)
        for i, vec in enumerate((bp, bm, b1, b2)):
            nc.scalar.dma_start(bias_rows[i * CB : (i + 1) * CB, :], vec.rearrange("(b p) o -> b (p o)", p=P))
        ident_f = held.tile([P, P], F32, name="ident_f")
        make_identity(nc, ident_f[:])
        bias_ps = psum_t.tile([P, BANK], F32, name="bias_ps", tag="t")
        nc.tensor.transpose(bias_ps[:, 0:BIAS_ROWS], bias_rows[:], ident_f[0:BIAS_ROWS, 0:BIAS_ROWS])
        bias_cols = held.tile([P, 4 * CB], F32, name="bias_cols")
        nc.vector.tensor_copy(bias_cols[:], bias_ps[:, 0 : 4 * CB])
        bp_t, bm_t, b1_t, b2_t = [bias_cols[:, i * CB : (i + 1) * CB] for i in range(4)]

        with tc.tile_pool(name="table", bufs=1) as table:
            emb_t = [table.tile([P, S], F32, name=f"emb{c}") for c in range(CB)]
            pos_t = [table.tile([P, N], F32, name=f"pos{c}") for c in range(CB)]
            for c in range(CB):
                if c == CB - 2:
                    nc.sync.dma_start(emb_t[c][:, 0 : S // 2], embed[blk(c), 0 : S // 2])
                    nc.sync.dma_start(wp_t[:, 0 : CB - 1, :], wp[0 : (CB - 1) * P, :].rearrange("(b p) d -> p b d", p=P))
                    nc.sync.dma_start(emb_t[c][:, S // 2 : S], embed[blk(c), S // 2 : S])
                else:
                    nc.sync.dma_start(emb_t[c][:], embed[blk(c), :])
                if c < CB - 1:
                    nc.sync.dma_start(pos_t[c][:], pos[blk(c), :])
                else:
                    for t0 in range(0, N, BANK // 2):
                        nc.sync.dma_start(pos_t[c][:, t0 : t0 + BANK // 2], pos[blk(c), t0 : t0 + BANK // 2])
                    nc.sync.dma_start(wp_t[:, c, :], wp[blk(c), :])
            for i in range(2):
                nc.sync.dma_start(
                    wm_t[:, 2 * i * CB : 2 * (i + 1) * CB, :], wm[2 * i * C : 2 * (i + 1) * C, :].rearrange("(b p) d -> p b d", p=P)
                )
            nc.sync.dma_start(w1_t[:], w1.rearrange("(b p) d -> p b d", p=P))
            nc.sync.dma_start(w2_t[:], w2.rearrange("(b p) d -> p b d", p=P))

            def borrowed_bank(i, name):
                if i < S_BANKS:
                    return psum_s.tile([P, BANK], F32, name=name, tag="s")
                return psum_t.tile([P, BANK], F32, name=name, tag="t")

            p_ps = [[borrowed_bank(hf * CB + d, f"p_ps{d}_{hf}") for hf in range(NH)] for d in range(CB)]
            for c in range(CB):
                width = BANK // 2 if c == CB - 1 else BANK
                for t0 in range(0, N, width):
                    cols = slice(t0, t0 + width)
                    picked = emb_t[c][:].indirect(offsets[:, t0 // 16 : (t0 + width) // 16])
                    nc.vector.tensor_tensor(h[c][:, cols], picked, pos_t[c][:, cols], ADD)
                    nc.scalar.copy(h_bf[c][:, cols], h[c][:, cols])
                    hf, b0 = divmod(t0, BANK)
                    for d in range(CB):
                        nc.tensor.matmul(
                            p_ps[d][hf][:, b0 : b0 + width], wp_t[:, c, blk(d)], h_bf[c][:, cols],
                            start=(c == 0), stop=(c == CB - 1 and b0 + width == BANK),
                        )
            for hf in range(NH):
                for d in range(CB):
                    if d % 2 == 0:
                        nc.scalar.activation(p_bf[d][:, half(hf)], p_ps[d][hf][:], FUNC.Identity, bias=bp_t[:, d : d + 1])
                    else:
                        nc.vector.tensor_scalar(p_bf[d][:, half(hf)], p_ps[d][hf][:], bp_t[:, d : d + 1], None, op0=ADD)

        with (
            tc.tile_pool(name="acts", bufs=1) as acts,
            tc.tile_pool(name="work", bufs=3) as work,
        ):
            pair01 = acts.tile([P, CB, C], F32, name="pair01")
            pair23 = acts.tile([P, CB, C], F32, name="pair23", tag="pair")
            wms = acts.tile([P, CB, C], BF16, name="wms")
            for d0 in range(0, CB, CB // 2):
                part = [slice(k * CB + d0, k * CB + d0 + CB // 2) for k in range(HEADS)]
                ds = part[0]
                nc.gpsimd.tensor_tensor(pair01[:, ds, :], wm_t[:, part[0], :], wm_t[:, part[1], :], ADD)
                nc.gpsimd.tensor_tensor(pair23[:, ds, :], wm_t[:, part[2], :], wm_t[:, part[3], :], ADD)
                nc.gpsimd.tensor_tensor(wms[:, ds, :], pair01[:, ds, :], pair23[:, ds, :], ADD)
            w1_pairs = acts.tile([P, CB, C], F32, name="w1_pairs", tag="pair")
            w1_sum = acts.tile([P, C], BF16, name="w1_sum")
            nc.gpsimd.tensor_tensor(w1_pairs[:, 0 : CB // 2, :], w1_t[:, 0 : CB // 2, :], w1_t[:, CB // 2 : CB, :], ADD)
            nc.gpsimd.tensor_tensor(w1_sum[:], w1_pairs[:, 0, :], w1_pairs[:, 1, :], ADD)

            def whole_array_norm(stats, pieces, tag):
                tot = psum_t.tile([P, BANK], F32, name="tot", tag="t")
                nc.tensor.matmul(tot[:, 0 : 2 * pieces], mean_w[:], stats[:].rearrange("p s g -> p (s g)"), start=True, stop=True)
                mom = small.tile([P, 2], F32, name="mom" + tag)
                nc.vector.tensor_reduce(mom[:], tot[:, 0 : 2 * pieces].rearrange("p (s g) -> p s g", s=2), axis=X, op=ADD)
                neg_var = small.tile([P, 1], F32, name="neg_var" + tag)
                nc.vector.tensor_scalar(neg_var[:], mom[:, 0:1], mom[:, 0:1], mom[:, 1:2], op0=MULT, op1=ADD)
                rho = small.tile([P, 1], F32, name="rho" + tag)
                nc.scalar.activation(rho[:], neg_var[:], FUNC.Abs_reciprocal_sqrt, bias=eps_t[:], scale=-1.0)
                return mom[:, 0:1], rho[:]

            vT = [acts.tile([P, C], BF16, name=f"vT{tb}") for tb in range(NB)]
            aT = [acts.tile([P, NB, BANK], BF16, name=f"aT{hf}") for hf in range(NH)]

            kept = acts.tile([P, NB, BANK], F32, name="kept")
            top_late = acts.tile([P, JB], F32, name="top_late")
            e_of, sums_of, a_of = {}, {}, {}

            square = [acts.tile([P, BANK], F32, name=f"square{jb}") for jb in range(JB)]

            def products(bank, row_block, first, cols):
                for d in range(CB):
                    nc.tensor.matmul(
                        bank[:, first * P : BANK], p_bf[d][:, blk(row_block)], p_bf[d][:, cols], start=(d == 0), stop=(d == CB - 1)
                    )

            def scores_and_exp(jb):
                s_ps = [psum_s.tile([P, BANK], F32, name=f"s_ps{hf}", tag="s") for hf in range(NH)]
                tops = small.tile([P, NH], F32, name="tops")
                products(s_ps[0], jb, jb, slice(jb * P, BANK))
                products(s_ps[1], jb, 0, half(1))
                for i in range(jb):
                    nc.tensor.transpose(s_ps[0][:, blk(i)], square[i][:, blk(jb)], ident_f[:])
                nc.vector.tensor_scalar(square[jb][:], s_ps[0][:], 1.0, None, op0=MULT, op1=MAX, accum_out=tops[:, 0:1])
                nc.vector.tensor_scalar(kept[:, jb, :], s_ps[1][:], 1.0, None, op0=MULT, op1=MAX, accum_out=tops[:, 1:2])
                neg_top = small.tile([P, 1], F32, name="neg_top")
                nc.vector.tensor_scalar(neg_top[:], tops[:, 0:1], tops[:, 1:2], -SCALE, op0=MAX, op1=MULT)
                e_of[jb] = work.tile([P, N], F32, name="e")
                sums_of[jb] = small.tile([P, NH], F32, name="sums")
                for hf in range(NH):
                    nc.scalar.activation(
                        e_of[jb][:, half(hf)], s_ps[hf][:], FUNC.Exp, bias=neg_top[:], scale=SCALE,
                        accum_out=sums_of[jb][:, hf : hf + 1],
                    )

            def normalise(jb):
                total = small.tile([P, 1], F32, name="total")
                nc.vector.tensor_reduce(total[:], sums_of[jb][:], axis=X, op=ADD)
                inv = small.tile([P, 1], F32, name="inv")
                nc.vector.reciprocal(inv[:], total[:])
                a_of[jb] = acts.tile([P, N], BF16, name=f"a{jb}")
                nc.scalar.activation(a_of[jb][:], e_of[jb][:], FUNC.Identity, scale=inv[:])

            def transpose_weights(jb):
                a_tr = psum_t.tile([P, N], BF16, name="a_tr", tag="t")
                for tb in range(NB):
                    nc.tensor.transpose(a_tr[:, blk(tb)], a_of[jb][:, blk(tb)], ident[:])
                copy_out = nc.scalar.copy if jb % 2 == 0 else nc.vector.tensor_copy
                copy_out(aT[0][:, :, blk(jb)], a_tr[:].rearrange("p (t j) -> p t j", t=NB))

            def scores_kept(tb):
                s_ps = psum_s.tile([P, BANK], F32, name="s_ps", tag="s")
                b = tb - JB
                products(s_ps, tb, b, slice(tb * P, N))
                for i in range(b):
                    nc.tensor.transpose(s_ps[:, blk(i)], kept[:, JB + i, blk(b)], ident_f[:])
                nc.vector.tensor_scalar(
                    kept[:, tb, :], s_ps[:], 1.0, None, op0=MULT, op1=MAX, accum_out=top_late[:, b : b + 1]
                )

            def spread(bank, column):
                for b in range(JB):
                    nc.tensor.transpose(bank[:, blk(b)], column[:, b : b + 1].to_broadcast([P, P]), ident[:])

            def exp_kept(tb):
                diff = work.tile([P, BANK], F32, name="diff", tag="bank")
                nc.vector.tensor_tensor(diff[:], kept[:, tb, :], neg_tops_ps[:], ADD)
                nc.scalar.activation(aT[1][:, tb, :], diff[:], FUNC.Exp, scale=SCALE)

            v_ps_of = {}

            def v_products(tb, ds):
                if ds[0] == 0:
                    v_ps_of[tb] = psum_s.tile([P, BANK], F32, name="v_ps", tag="s")
                for d in ds:
                    nc.tensor.matmul(v_ps_of[tb][:], p_bf[d][:, blk(tb)], wms[:, d, :], start=(d == 0), stop=(d == CB - 1))
                if ds[-1] == CB - 1:
                    nc.scalar.copy(vT[tb][:], v_ps_of[tb][:])

            for step in range(JB):
                scores_and_exp(step)
                if step >= 1:
                    normalise(step - 1)
            for step in range(JB):
                scores_kept(JB + step)
                if step == 0:
                    normalise(JB - 1)
                transpose_weights(step)
            col_top = acts.tile([P, BANK], BF16, name="col_top")
            nc.vector.tensor_reduce(col_top[:], kept[:, 0:JB, :].rearrange("p t j -> p j t"), axis=X, op=MAX)
            for tb in range(V_OPEN):
                v_products(tb, range(0, CB // 2))
            col_ps = psum_s.tile([P, BANK], BF16, name="col_ps", tag="s")
            for b in range(JB):
                nc.tensor.transpose(col_ps[:, blk(b)], col_top[:, blk(b)], ident[:])
            top_early = acts.tile([P, JB], F32, name="top_early")
            nc.vector.tensor_reduce(top_early[:], col_ps[:].rearrange("p (b t) -> p b t", b=JB), axis=X, op=MAX)
            neg_tops = acts.tile([P, JB], BF16, name="neg_tops")
            for b in range(JB):
                nc.vector.tensor_scalar(
                    neg_tops[:, b : b + 1], top_early[:, b : b + 1], top_late[:, b : b + 1], -1.0, op0=MAX, op1=MULT
                )
            for tb in range(V_OPEN):
                v_products(tb, range(CB // 2, CB))
            neg_tops_ps = psum_s.tile([P, BANK], BF16, name="neg_tops_ps", tag="s")
            spread(neg_tops_ps, neg_tops)
            e_sum = None
            for tb in range(NB):
                if tb < NB - V_OPEN:
                    v_products(V_OPEN + tb, range(CB))
                exp_kept(tb)
                if tb > 0:
                    before = aT[1][:, 0, :] if tb == 1 else e_sum[:]
                    e_sum = work.tile([P, BANK], F32, name="e_sum", tag="col")
                    nc.gpsimd.tensor_tensor(e_sum[:], before, aT[1][:, tb, :], ADD)
            e_sum_hi = acts.tile([P, BANK], BF16, name="e_sum_hi")
            e_sum_lo = acts.tile([P, BANK], BF16, name="e_sum_lo")
            nc.gpsimd.tensor_copy(e_sum_hi[:], e_sum[:])
            nc.gpsimd.tensor_tensor(e_sum_lo[:], e_sum[:], e_sum_hi[:], SUB)

            colsum_ps = psum_t.tile([P, BANK], F32, name="colsum_ps", tag="t")
            for d in range(CB):
                nc.tensor.matmul(colsum_ps[:, d : d + 1], w1_sum[:, blk(d)], ones_bf[:, 0:1], start=True, stop=True)
            w1_colsum = acts.tile([P, CB], F32, name="w1_colsum")
            nc.vector.tensor_copy(w1_colsum[:], colsum_ps[:, 0:CB])

            y = [acts.tile([P, N], F32, name=f"y{c}") for c in range(CB)]
            y_stats = acts.tile([P, 2, GROUPS], F32, name="y_stats")
            yc_bf = [acts.tile([P, N], BF16, name=f"yc_bf{c}") for c in range(CB)]
            neg_m0 = acts.tile([P, 1], F32, name="neg_m0")

            def centre(hf, c):
                nc.scalar.activation(yc_bf[c][:, half(hf)], y[c][:, half(hf)], FUNC.Identity, bias=neg_m0[:])

            inv_b = acts.tile([P, BANK], F32, name="inv_b")
            for g in range(GROUPS):
                hf, c = divmod(g, CB)
                y_ps = psum_s.tile([P, BANK], F32, name="y_ps", tag="s")
                for tb in range(NB):
                    nc.tensor.matmul(y_ps[:], vT[tb][:, blk(c)], aT[hf][:, tb, :], start=(tb == 0), stop=(tb == NB - 1))
                if g == CB:
                    sum_ps = psum_s.tile([P, BANK], F32, name="sum_ps", tag="s")
                    nc.tensor.matmul(sum_ps[:], ones_bf[:], e_sum_hi[:], start=True, stop=False)
                    nc.tensor.matmul(sum_ps[:], ones_bf[:], e_sum_lo[:], start=False, stop=True)
                    nc.scalar.activation(inv_b[:], sum_ps[:], FUNC.Abs_reciprocal_sqrt)
                    nc.scalar.activation(inv_b[:], inv_b[:], FUNC.Square)
                    m0_ps = psum_t.tile([P, BANK], F32, name="m0_ps", tag="t")
                    nc.tensor.matmul(m0_ps[:, 0:CB], half_mean_w[:], y_stats[:, 0, 0:CB], start=True, stop=True)
                    nc.vector.tensor_reduce(neg_m0[:], m0_ps[:, 0:CB], axis=X, op=ADD)
                    for c0 in range(CB):
                        centre(0, c0)
                if hf == 0:
                    y_in = y_ps
                else:
                    y_in = work.tile([P, BANK], F32, name="y_in", tag="bank")
                    nc.vector.tensor_tensor(y_in[:], y_ps[:], inv_b[:], MULT)
                nc.vector.scalar_tensor_tensor(
                    y[c][:, half(hf)], y_in[:], bm_t[:, c : c + 1], h[c][:, half(hf)], op0=ADD, op1=ADD,
                    accum_out=y_stats[:, 0, g : g + 1],
                )
                y_sq = work.tile([P, BANK], BF16, name="y_sq")
                nc.scalar.activation(y_sq[:], y[c][:, half(hf)], FUNC.Square, accum_out=y_stats[:, 1, g : g + 1])
                if hf == 1:
                    centre(1, c)

            def w1_products(g):
                hf, d = divmod(g, CB)
                f_ps = psum_s.tile([P, BANK], F32, name="f_ps", tag="s")
                for c in range(CB):
                    nc.tensor.matmul(f_ps[:], w1_t[:, c, blk(d)], yc_bf[c][:, half(hf)], start=(c == 0), stop=(c == CB - 1))
                return f_ps

            f_early = [w1_products(g) for g in range(AHEAD)]

            neg_mean1, rho1 = whole_array_norm(y_stats, GROUPS, "1")
            sigma = small.tile([P, 1], F32, name="sigma")
            nc.vector.reciprocal(sigma[:], rho1)
            shift = small.tile([P, 1], F32, name="shift")
            nc.vector.tensor_scalar(shift[:], neg_mean1, rho1, None, op0=MULT)
            drift = small.tile([P, 1], F32, name="drift")
            nc.vector.tensor_scalar(drift[:], neg_mean1, neg_m0[:], None, op0=SUB)
            drift_colsum = small.tile([P, CB], F32, name="drift_colsum")
            nc.vector.tensor_scalar(drift_colsum[:], w1_colsum[:], drift[:], None, op0=MULT)
            f_bias = small.tile([P, CB], F32, name="f_bias")
            nc.vector.scalar_tensor_tensor(f_bias[:], b1_t, sigma[:], drift_colsum[:], op0=MULT, op1=ADD)
            shift_b2 = small.tile([P, CB], F32, name="shift_b2")
            nc.vector.tensor_scalar(shift_b2[:], b2_t, shift[:], None, op0=ADD)

            sf_bf = [acts.tile([P, N], BF16, name=f"sf_bf{d}") for d in range(CB)]
            for g in range(GROUPS):
                hf, d = divmod(g, CB)
                f_ps = f_early[g] if g < AHEAD else w1_products(g)
                if d % 2 == 0:
                    nc.scalar.activation(sf_bf[d][:, half(hf)], f_ps[:], FUNC.Relu, bias=f_bias[:, d : d + 1])
                else:
                    nc.vector.tensor_scalar(sf_bf[d][:, half(hf)], f_ps[:], f_bias[:, d : d + 1], 0.0, op0=ADD, op1=MAX)

            h1_b2 = [acts.tile([P, N], F32, name=f"h1_b2_{c}") for c in range(CB)]
            for c in range(CB):
                nc.gpsimd.tensor_scalar(h1_b2[c][:], y[c][:], rho1, shift_b2[:, c : c + 1], op0=MULT, op1=ADD)

            z = [held.tile([P, N], F32, name=f"z{c}", tag=f"h{c}") for c in range(CB)]
            z_pieces = [(g % CB, (g // CB) * BANK, BANK) for g in range(GROUPS - 1)]
            z_pieces += [(CB - 1, N - BANK + i * (BANK // 2), BANK // 2) for i in range(2)]
            z_stats = acts.tile([P, 2, len(z_pieces)], F32, name="z_stats")
            for i, (c, t0, width) in enumerate(z_pieces):
                cols = slice(t0, t0 + width)
                z_ps = psum_s.tile([P, BANK], F32, name="z_ps", tag="s")
                for d in range(CB):
                    nc.tensor.matmul(z_ps[:, 0:width], w2_t[:, d, blk(c)], sf_bf[d][:, cols], start=(d == 0), stop=(d == CB - 1))
                nc.vector.scalar_tensor_tensor(
                    z[c][:, cols], z_ps[:, 0:width], rho1, h1_b2[c][:, cols], op0=MULT, op1=ADD,
                    accum_out=z_stats[:, 0, i : i + 1],
                )
                z_sq = work.tile([P, BANK], BF16, name="z_sq")
                nc.scalar.activation(z_sq[:, 0:width], z[c][:, cols], FUNC.Square, accum_out=z_stats[:, 1, i : i + 1])

            neg_mean2, rho2 = whole_array_norm(z_stats, len(z_pieces), "2")
            res = [acts.tile([P, N], F32, name=f"res{c}", tag=f"y{c}") for c in range(CB)]
            for c in range(CB):
                width = BANK if c < CB // 2 else N
                for t0 in range(0, N, width):
                    cols = slice(t0, t0 + width)
                    nc.vector.tensor_scalar(res[c][:, cols], z[c][:, cols], neg_mean2, rho2, op0=ADD, op1=MULT)
                    nc.sync.dma_start(out[blk(c), cols], res[c][:, cols])
